import numpy as np
import ml_dtypes


def mxq(x, axis, fmt="e4m3"):
    dtype, down = {"e4m3": (ml_dtypes.float8_e4m3fn, 7), "e5m2": (ml_dtypes.float8_e5m2, 14)}[fmt]
    v = np.moveaxis(np.asarray(x, np.float32).astype(ml_dtypes.bfloat16).astype(np.float64), axis, -1)
    blocks = v.reshape(v.shape[:-1] + (-1, 32))
    amax = np.abs(blocks).max(-1, keepdims=True)
    byte = np.maximum(np.where(amax > 0, np.frexp(amax)[1] - 1 + 127, 0) - down, 1)
    scale = np.exp2(byte - 127.0)
    codes = (blocks / scale).astype(np.float32).astype(dtype).astype(np.float64)
    return np.moveaxis((codes * scale).reshape(v.shape), -1, axis)


BF16 = ml_dtypes.bfloat16


def bf(x):
    return np.asarray(x, np.float32).astype(BF16)


def f64(x):
    return np.asarray(x).astype(np.float64)


B, N, D = 32, 512, 256
R = D // 64


def setup_inputs():
    z = np.random.standard_normal((B, N, R))
    a = np.random.standard_normal((B, R, D))
    noise = np.random.standard_normal((B, N, D))
    return {"x": bf(3.0 * (z @ a / np.sqrt(R) + 0.5 * noise))}


def reference(x):
    xf = f64(x)
    norm = np.sqrt(np.sum(xf * xf, axis=2, keepdims=True))
    scores = (xf @ xf.transpose(0, 2, 1)) / (norm * norm.transpose(0, 2, 1))
    e = np.exp(scores - scores.max(-1, keepdims=True))
    return (mxq(e, 2, "e4m3") @ mxq(xf, 1, "e4m3")) / e.sum(-1, keepdims=True)

@@ -1,0 +1,228 @@
+from contextlib import ExitStack
+
+import concourse.bass as bass
+import concourse.mybir as mybir
+import concourse.tile as tile
+from concourse.masks import make_identity
+
+F32 = mybir.dt.float32
+BF16 = mybir.dt.bfloat16
+U32 = mybir.dt.uint32
+U8 = mybir.dt.uint8
+FP8X4 = mybir.dt.float8_e4m3fn_x4
+ALU = mybir.AluOpType
+ACTF = mybir.ActivationFunctionType
+
+P = 128
+B, N, D = 32, 512, 256
+T = N // P
+FLOPS = 2 * (2 * B * N * N * D)
+MANUAL = False
+LOAD_GROUPS = [1, 1, 2, 4, 4, 4, 4, 4, 4, 4]
+
+
+def tile_scaleddotproductattention_t_kernel(tc, x, out):
+    nc = tc.nc
+    with ExitStack() as ctx:
+        const = ctx.enter_context(tc.tile_pool(name="const", bufs=1))
+        xres = ctx.enter_context(tc.tile_pool(name="xres", bufs=1))
+        small = ctx.enter_context(tc.tile_pool(name="small", bufs=6))
+        work2 = ctx.enter_context(tc.tile_pool(name="work2", bufs=2))
+        work3 = ctx.enter_context(tc.tile_pool(name="work3", bufs=3))
+        spool = ctx.enter_context(tc.tile_pool(name="spool", bufs=4))
+        gps = ctx.enter_context(tc.psum_pool(name="gps", bufs=4))
+        tps = ctx.enter_context(tc.psum_pool(name="tps", bufs=1))
+        ops = ctx.enter_context(tc.psum_pool(name="ops", bufs=1))
+        if MANUAL:
+            ctx.enter_context(tc.manual_schedule())
+
+        xb3 = []
+        xbw = []
+        b0 = 0
+        for g, nb in enumerate(LOAD_GROUPS):
+            xt = xres.tile([P, nb * T * D], BF16, name="x%d" % g)
+            nc.sync.dma_start(
+                out=xt[:].rearrange("p (k n) -> p k n", n=T * D),
+                in_=x[b0 : b0 + nb].rearrange("b (p t) d -> p b (t d)", t=T),
+            )
+            v3 = xt[:].rearrange("p (k t d) -> p k t d", t=T, d=D)
+            vw = xt[:].bitcast(F32)
+            for k in range(nb):
+                xb3.append(v3[:, k])
+                xbw.append(vw[:, k * (T * D // 2) : (k + 1) * (T * D // 2)])
+            b0 += nb
+
+        ident = const.tile([P, P], F32, name="ident")
+        make_identity(nc, ident[:])
+        mhalf = const.tile([P, T], F32, name="mhalf")
+        nc.vector.memset(mhalf[:], -0.5)
+
+        rn = {}
+        xT = {}
+        RI = {}
+        xq = {}
+        G = {}
+        E = {}
+        rs = {}
+        eq = {}
+        rinv = {}
+
+        def stage_norm(b):
+            nsq = small.tile([P, T], F32, name="nsq")
+            for t in range(T):
+                junk = work2.tile([P, D], BF16, name="junk")
+                nc.scalar.activation(
+                    out=junk[:], in_=xb3[b][:, t, :], func=ACTF.Square, accum_out=nsq[:, t : t + 1]
+                )
+            r = small.tile([P, T], F32, name="rn")
+            nc.gpsimd.tensor_tensor(out=r[:], in0=nsq[:], in1=mhalf[:], op=ALU.pow)
+            rn[b] = r
+
+        def pe_xt(b):
+            xtp = tps.tile([P, T, P], F32, name="xtp")
+            for t in range(T):
+                nc.tensor.transpose(xtp[:, t, :], xbw[b][:, t * P : (t + 1) * P], ident[:])
+            return xtp
+
+        def act_xt(b, xtp):
+            xs = work3.tile([P, T * P], F32, name="xT")
+            nc.scalar.copy(out=xs[:], in_=xtp[:].rearrange("q t p -> q (t p)"))
+            xT[b] = xs
+
+        def pe_ri(b):
+            rip = tps.tile([P, T, P], F32, name="rip")
+            for c in range(T):
+                nc.tensor.transpose(rip[:, c, :], rn[b][:, c : c + 1].to_broadcast([P, P]), ident[:])
+            return rip
+
+        def act_ri(b, rip):
+            ri = work2.tile([P, T * P], F32, name="RI")
+            nc.scalar.copy(out=ri[:], in_=rip[:].rearrange("q t p -> q (t p)"))
+            RI[b] = ri
+
+        def pe_scores(b):
+            xv = xT[b][:].bitcast(BF16).rearrange("q (n e) -> q n e", e=2)
+            G[b] = []
+            for t in range(T):
+                g = gps.tile([P, N], F32, name="g")
+                for e in range(2):
+                    nc.tensor.matmul(
+                        g[:],
+                        lhsT=xv[:, t * P : (t + 1) * P, e],
+                        rhs=xv[:, :, e],
+                        start=(e == 0),
+                        stop=(e == 1),
+                    )
+                G[b].append(g)
+
+        def scale_exp(b):
+            et = work2.tile([P, T, N], BF16, name="E")
+            r = small.tile([P, T], F32, name="rs")
+            for t in range(T):
+                s = spool.tile([P, N], F32, name="s")
+                nc.vector.scalar_tensor_tensor(
+                    out=s[:], in0=G[b][t][:], scalar=rn[b][:, t : t + 1], in1=RI[b][:],
+                    op0=ALU.mult, op1=ALU.mult,
+                )
+                nc.scalar.activation(
+                    out=et[:, t, :], in_=s[:], func=ACTF.Exp, bias=-1.0, scale=1.0,
+                    accum_out=r[:, t : t + 1],
+                )
+            E[b] = et
+            rs[b] = r
+
+        def x_regroup(b):
+            xg = work2.tile([P, D, T], BF16, name="xg", align_bytes=64)
+            nc.vector.tensor_copy(
+                out=xg[:].rearrange("p (c i) t -> p c t i", i=4),
+                in_=xb3[b].rearrange("p t (c i) -> p c t i", i=4),
+            )
+            return xg
+
+        def x_quant(b, xg):
+            w = work3.tile([P, D], U32, name="xq", align_bytes=64)
+            sc = work3.tile([P, D], U8, name="xsc", align_bytes=64)
+            nc.vector.quantize_mx(
+                out=w[:].bitcast(FP8X4), scales=sc[:], in_=xg[:].rearrange("p d t -> p (d t)")
+            )
+            xq[b] = (w, sc)
+
+        def e_regroup(b):
+            eg = work2.tile([P, N, T], BF16, name="eg", align_bytes=64)
+            nc.vector.tensor_copy(
+                out=eg[:].rearrange("p (c i) t -> p c t i", i=4),
+                in_=E[b][:].rearrange("p t (c i) -> p c t i", i=4),
+            )
+            return eg
+
+        def e_quant(b, eg):
+            w = work2.tile([P, N], U32, name="eq", align_bytes=64)
+            sc = work2.tile([P, N], U8, name="esc", align_bytes=64)
+            nc.vector.quantize_mx(
+                out=w[:].bitcast(FP8X4), scales=sc[:], in_=eg[:].rearrange("p i t -> p (i t)")
+            )
+            eq[b] = (w, sc)
+
+        def recip(b):
+            r = small.tile([P, T], F32, name="rinv")
+            nc.vector.reciprocal(out=r[:], in_=rs[b][:])
+            rinv[b] = r
+
+        def pe_mx(b):
+            w, sc = eq[b]
+            xw, xsc = xq[b]
+            banks = []
+            for h in range(2):
+                o = ops.tile([P, 2, D], F32, name="op%d" % h)
+                for k in range(2):
+                    c = 2 * h + k
+                    nc.tensor.matmul_mx(
+                        out=o[:, k, :],
+                        lhsT=w[:, c * P : (c + 1) * P].bitcast(FP8X4),
+                        lhsT_scale=sc[:, c * P : (c + 1) * P],
+                        rhs=xw[:].bitcast(FP8X4),
+                        rhs_scale=xsc[:],
+                        start=True,
+                        stop=True,
+                    )
+                banks.append(o)
+            return banks
+
+        pend = {}
+        for b in range(-3, B + 1):
+            if 0 <= b < B:
+                scale_exp(b)
+            if 0 <= b - 1 < B:
+                pend["op"] = pe_mx(b - 1)
+            if 0 <= b + 2 < B:
+                pend["xtp"] = pe_xt(b + 2)
+            if 0 <= b + 1 < B:
+                pend["rip"] = pe_ri(b + 1)
+                pe_scores(b + 1)
+                act_ri(b + 1, pend["rip"])
+            if 0 <= b + 2 < B:
+                act_xt(b + 2, pend["xtp"])
+            if 0 <= b + 1 < B:
+                pend["xg"] = x_regroup(b + 1)
+            if 0 <= b - 1 < B:
+                bb = b - 1
+                o = work3.tile([P, T, D], F32, name="o")
+                nc.vector.tensor_tensor(
+                    out=o[:, 2:4, :], in0=pend["op"][1][:],
+                    in1=rinv[bb][:, 2:4].unsqueeze(2).to_broadcast([P, 2, D]), op=ALU.mult,
+                )
+                for c in range(2):
+                    nc.scalar.activation(
+                        out=o[:, c, :], in_=pend["op"][0][:, c, :], func=ACTF.Copy,
+                        scale=rinv[bb][:, c : c + 1],
+                    )
+                nc.sync.dma_start(out=out[bb].rearrange("(r c) d -> r c d", c=T), in_=o[:])
+            if 0 <= b < B:
+                pend["eg"] = e_regroup(b)
+            if 0 <= b + 1 < B:
+                x_quant(b + 1, pend["xg"])
+            if 0 <= b < B:
+                recip(b)
+                e_quant(b, pend["eg"])
+            if 0 <= b + 3 < B:
+                stage_norm(b + 3)

@@ -17,7 +17,7 @@ P = 128
 B, N, D = 32, 512, 256
 T = N // P
 FLOPS = 2 * (2 * B * N * N * D)
-MANUAL = False
+MANUAL = True
 LOAD_GROUPS = [1, 1, 2, 4, 4, 4, 4, 4, 4, 4]
 
 
@@ -26,7 +26,9 @@ def tile_scaleddotproductattention_t_kernel(tc, x, out):
     with ExitStack() as ctx:
         const = ctx.enter_context(tc.tile_pool(name="const", bufs=1))
         xres = ctx.enter_context(tc.tile_pool(name="xres", bufs=1))
-        small = ctx.enter_context(tc.tile_pool(name="small", bufs=6))
+        small = ctx.enter_context(tc.tile_pool(name="small", bufs=8))
+        one = ctx.enter_context(tc.tile_pool(name="one", bufs=1))
+        work5 = ctx.enter_context(tc.tile_pool(name="work5", bufs=5))
         work2 = ctx.enter_context(tc.tile_pool(name="work2", bufs=2))
         work3 = ctx.enter_context(tc.tile_pool(name="work3", bufs=3))
         spool = ctx.enter_context(tc.tile_pool(name="spool", bufs=4))
@@ -116,7 +118,7 @@ def tile_scaleddotproductattention_t_kernel(tc, x, out):
                 G[b].append(g)
 
         def scale_exp(b):
-            et = work2.tile([P, T, N], BF16, name="E")
+            et = work3.tile([P, T, N], BF16, name="E")
             r = small.tile([P, T], F32, name="rs")
             for t in range(T):
                 s = spool.tile([P, N], F32, name="s")
@@ -140,18 +142,18 @@ def tile_scaleddotproductattention_t_kernel(tc, x, out):
             return xg
 
         def x_quant(b, xg):
-            w = work3.tile([P, D], U32, name="xq", align_bytes=64)
-            sc = work3.tile([P, D], U8, name="xsc", align_bytes=64)
+            w = work5.tile([P, D], U32, name="xq", align_bytes=64)
+            sc = work5.tile([P, D], U8, name="xsc", align_bytes=64)
             nc.vector.quantize_mx(
                 out=w[:].bitcast(FP8X4), scales=sc[:], in_=xg[:].rearrange("p d t -> p (d t)")
             )
             xq[b] = (w, sc)
 
         def e_regroup(b):
-            eg = work2.tile([P, N, T], BF16, name="eg", align_bytes=64)
-            nc.vector.tensor_copy(
-                out=eg[:].rearrange("p (c i) t -> p c t i", i=4),
-                in_=E[b][:].rearrange("p t (c i) -> p c t i", i=4),
+            eg = one.tile([P, N, T], BF16, name="eg", align_bytes=64)
+            nc.gpsimd.tensor_scalar(
+                out=eg[:], in0=E[b][:].rearrange("p t i -> p i t"),
+                scalar1=1.0, scalar2=0.0, op0=ALU.mult, op1=ALU.add,
             )
             return eg
 
@@ -188,41 +190,45 @@ def tile_scaleddotproductattention_t_kernel(tc, x, out):
                 banks.append(o)
             return banks
 
-        pend = {}
-        for b in range(-3, B + 1):
-            if 0 <= b < B:
+        xgs = {}
+        egs = {}
+
+        def live(b):
+            return 0 <= b < B
+
+        for b in range(-4, B + 2):
+            if live(b + 2):
+                xgs[b + 2] = x_regroup(b + 2)
+            if live(b + 1):
+                x_quant(b + 1, xgs[b + 1])
+            if live(b - 2):
+                e_quant(b - 2, egs[b - 2])
+            if live(b + 2):
+                xtp = pe_xt(b + 2)
+            if live(b + 1):
+                rip = pe_ri(b + 1)
+            if live(b - 2):
+                banks = pe_mx(b - 2)
+            if live(b - 1):
+                egs[b - 1] = e_regroup(b - 1)
+            if live(b):
                 scale_exp(b)
-            if 0 <= b - 1 < B:
-                pend["op"] = pe_mx(b - 1)
-            if 0 <= b + 2 < B:
-                pend["xtp"] = pe_xt(b + 2)
-            if 0 <= b + 1 < B:
-                pend["rip"] = pe_ri(b + 1)
+            if live(b + 1):
                 pe_scores(b + 1)
-                act_ri(b + 1, pend["rip"])
-            if 0 <= b + 2 < B:
-                act_xt(b + 2, pend["xtp"])
-            if 0 <= b + 1 < B:
-                pend["xg"] = x_regroup(b + 1)
-            if 0 <= b - 1 < B:
-                bb = b - 1
+            if live(b - 2):
+                bb = b - 2
+                recip(bb)
                 o = work3.tile([P, T, D], F32, name="o")
-                nc.vector.tensor_tensor(
-                    out=o[:, 2:4, :], in0=pend["op"][1][:],
-                    in1=rinv[bb][:, 2:4].unsqueeze(2).to_broadcast([P, 2, D]), op=ALU.mult,
-                )
-                for c in range(2):
-                    nc.scalar.activation(
-                        out=o[:, c, :], in_=pend["op"][0][:, c, :], func=ACTF.Copy,
-                        scale=rinv[bb][:, c : c + 1],
+                for h in range(2):
+                    nc.vector.tensor_tensor(
+                        out=o[:, 2 * h : 2 * h + 2, :], in0=banks[h][:],
+                        in1=rinv[bb][:, 2 * h : 2 * h + 2].unsqueeze(2).to_broadcast([P, 2, D]),
+                        op=ALU.mult,
                     )
                 nc.sync.dma_start(out=out[bb].rearrange("(r c) d -> r c d", c=T), in_=o[:])
-            if 0 <= b < B:
-                pend["eg"] = e_regroup(b)
-            if 0 <= b + 1 < B:
-                x_quant(b + 1, pend["xg"])
-            if 0 <= b < B:
-                recip(b)
-                e_quant(b, pend["eg"])
-            if 0 <= b + 3 < B:
-                stage_norm(b + 3)
+            if live(b + 1):
+                act_ri(b + 1, rip)
+            if live(b + 2):
+                act_xt(b + 2, xtp)
+            if live(b + 4):
+                stage_norm(b + 4)

@@ -18,6 +18,9 @@ B, N, D = 32, 512, 256
 T = N // P
 FLOPS = 2 * (2 * B * N * N * D)
 MANUAL = True
+LX = 6
+LN = 4
+TAIL_A = 4
 LOAD_GROUPS = [1, 1, 2, 4, 4, 4, 4, 4, 4, 4]
 
 
@@ -28,7 +31,7 @@ def tile_scaleddotproductattention_t_kernel(tc, x, out):
         xres = ctx.enter_context(tc.tile_pool(name="xres", bufs=1))
         small = ctx.enter_context(tc.tile_pool(name="small", bufs=8))
         one = ctx.enter_context(tc.tile_pool(name="one", bufs=1))
-        work5 = ctx.enter_context(tc.tile_pool(name="work5", bufs=5))
+        work5 = ctx.enter_context(tc.tile_pool(name="work5", bufs=10))
         work2 = ctx.enter_context(tc.tile_pool(name="work2", bufs=2))
         work3 = ctx.enter_context(tc.tile_pool(name="work3", bufs=3))
         spool = ctx.enter_context(tc.tile_pool(name="spool", bufs=4))
@@ -60,6 +63,7 @@ def tile_scaleddotproductattention_t_kernel(tc, x, out):
         nc.vector.memset(mhalf[:], -0.5)
 
         rn = {}
+        nsq = {}
         xT = {}
         RI = {}
         xq = {}
@@ -69,15 +73,18 @@ def tile_scaleddotproductattention_t_kernel(tc, x, out):
         eq = {}
         rinv = {}
 
-        def stage_norm(b):
-            nsq = small.tile([P, T], F32, name="nsq")
+        def sumsq(b):
+            q = small.tile([P, T], F32, name="nsq")
             for t in range(T):
                 junk = work2.tile([P, D], BF16, name="junk")
                 nc.scalar.activation(
-                    out=junk[:], in_=xb3[b][:, t, :], func=ACTF.Square, accum_out=nsq[:, t : t + 1]
+                    out=junk[:], in_=xb3[b][:, t, :], func=ACTF.Square, accum_out=q[:, t : t + 1]
                 )
+            nsq[b] = q
+
+        def rsqrt(b):
             r = small.tile([P, T], F32, name="rn")
-            nc.gpsimd.tensor_tensor(out=r[:], in0=nsq[:], in1=mhalf[:], op=ALU.pow)
+            nc.gpsimd.tensor_tensor(out=r[:], in0=nsq[b][:], in1=mhalf[:], op=ALU.pow)
             rn[b] = r
 
         def pe_xt(b):
@@ -149,12 +156,18 @@ def tile_scaleddotproductattention_t_kernel(tc, x, out):
             )
             xq[b] = (w, sc)
 
-        def e_regroup(b):
+        def e_regroup(b, on_vector):
             eg = one.tile([P, N, T], BF16, name="eg", align_bytes=64)
-            nc.gpsimd.tensor_scalar(
-                out=eg[:], in0=E[b][:].rearrange("p t i -> p i t"),
-                scalar1=1.0, scalar2=0.0, op0=ALU.mult, op1=ALU.add,
-            )
+            if on_vector:
+                nc.vector.tensor_copy(
+                    out=eg[:].rearrange("p (c i) t -> p c t i", i=4),
+                    in_=E[b][:].rearrange("p t (c i) -> p c t i", i=4),
+                )
+            else:
+                nc.gpsimd.tensor_scalar(
+                    out=eg[:], in0=E[b][:].rearrange("p t i -> p i t"),
+                    scalar1=1.0, scalar2=0.0, op0=ALU.mult, op1=ALU.add,
+                )
             return eg
 
         def e_quant(b, eg):
@@ -196,11 +209,29 @@ def tile_scaleddotproductattention_t_kernel(tc, x, out):
         def live(b):
             return 0 <= b < B
 
-        for b in range(-4, B + 2):
-            if live(b + 2):
-                xgs[b + 2] = x_regroup(b + 2)
-            if live(b + 1):
-                x_quant(b + 1, xgs[b + 1])
+        def finish(bb, banks):
+            recip(bb)
+            o = work3.tile([P, T, D], F32, name="o")
+            for h in range(2):
+                if h == 0 and bb >= B - TAIL_A:
+                    for c in range(2):
+                        nc.scalar.activation(
+                            out=o[:, c, :], in_=banks[0][:, c, :], func=ACTF.Copy,
+                            scale=rinv[bb][:, c : c + 1],
+                        )
+                else:
+                    nc.vector.tensor_tensor(
+                        out=o[:, 2 * h : 2 * h + 2, :], in0=banks[h][:],
+                        in1=rinv[bb][:, 2 * h : 2 * h + 2].unsqueeze(2).to_broadcast([P, 2, D]),
+                        op=ALU.mult,
+                    )
+            nc.sync.dma_start(out=out[bb].rearrange("(r c) d -> r c d", c=T), in_=o[:])
+
+        for b in range(-max(LX, LN), B + 2):
+            if live(b + LX):
+                xgs[b + LX] = x_regroup(b + LX)
+            if live(b + LX - 1):
+                x_quant(b + LX - 1, xgs[b + LX - 1])
             if live(b - 2):
                 e_quant(b - 2, egs[b - 2])
             if live(b + 2):
@@ -210,25 +241,18 @@ def tile_scaleddotproductattention_t_kernel(tc, x, out):
             if live(b - 2):
                 banks = pe_mx(b - 2)
             if live(b - 1):
-                egs[b - 1] = e_regroup(b - 1)
+                egs[b - 1] = e_regroup(b - 1, b - 1 == B - 1)
+            if live(b + LN - 1):
+                rsqrt(b + LN - 1)
             if live(b):
                 scale_exp(b)
             if live(b + 1):
                 pe_scores(b + 1)
             if live(b - 2):
-                bb = b - 2
-                recip(bb)
-                o = work3.tile([P, T, D], F32, name="o")
-                for h in range(2):
-                    nc.vector.tensor_tensor(
-                        out=o[:, 2 * h : 2 * h + 2, :], in0=banks[h][:],
-                        in1=rinv[bb][:, 2 * h : 2 * h + 2].unsqueeze(2).to_broadcast([P, 2, D]),
-                        op=ALU.mult,
-                    )
-                nc.sync.dma_start(out=out[bb].rearrange("(r c) d -> r c d", c=T), in_=o[:])
+                finish(b - 2, banks)
             if live(b + 1):
                 act_ri(b + 1, rip)
             if live(b + 2):
                 act_xt(b + 2, xtp)
-            if live(b + 4):
-                stage_norm(b + 4)
+            if live(b + LN):
+                sumsq(b + LN)

@@ -210,7 +210,6 @@ def tile_scaleddotproductattention_t_kernel(tc, x, out):
             return 0 <= b < B
 
         def finish(bb, banks):
-            recip(bb)
             o = work3.tile([P, T, D], F32, name="o")
             for h in range(2):
                 if h == 0 and bb >= B - TAIL_A:
@@ -233,6 +232,7 @@ def tile_scaleddotproductattention_t_kernel(tc, x, out):
             if live(b + LX - 1):
                 x_quant(b + LX - 1, xgs[b + LX - 1])
             if live(b - 2):
+                recip(b - 2)
                 e_quant(b - 2, egs[b - 2])
             if live(b + 2):
                 xtp = pe_xt(b + 2)

@@ -20,7 +20,10 @@ FLOPS = 2 * (2 * B * N * N * D)
 MANUAL = True
 LX = 6
 LN = 4
-TAIL_A = 4
+TAIL_A = 6
+TAIL_A2 = 3
+HEAD_V = 3
+TAIL_V = 4
 LOAD_GROUPS = [1, 1, 2, 4, 4, 4, 4, 4, 4, 4]
 
 
@@ -105,8 +108,11 @@ def tile_scaleddotproductattention_t_kernel(tc, x, out):
             return rip
 
         def act_ri(b, rip):
-            ri = work2.tile([P, T * P], F32, name="RI")
-            nc.scalar.copy(out=ri[:], in_=rip[:].rearrange("q t p -> q (t p)"))
+            ri = work3.tile([P, T * P], F32, name="RI")
+            if b < HEAD_V or b >= B - TAIL_V:
+                nc.vector.tensor_copy(out=ri[:], in_=rip[:].rearrange("q t p -> q (t p)"))
+            else:
+                nc.scalar.copy(out=ri[:], in_=rip[:].rearrange("q t p -> q (t p)"))
             RI[b] = ri
 
         def pe_scores(b):
@@ -212,10 +218,11 @@ def tile_scaleddotproductattention_t_kernel(tc, x, out):
         def finish(bb, banks):
             o = work3.tile([P, T, D], F32, name="o")
             for h in range(2):
-                if h == 0 and bb >= B - TAIL_A:
-                    for c in range(2):
+                if bb >= B - (TAIL_A if h == 0 else TAIL_A2):
+                    for k in range(2):
+                        c = 2 * h + k
                         nc.scalar.activation(
-                            out=o[:, c, :], in_=banks[0][:, c, :], func=ACTF.Copy,
+                            out=o[:, c, :], in_=banks[h][:, k, :], func=ACTF.Copy,
                             scale=rinv[bb][:, c : c + 1],
                         )
                 else:
@@ -248,11 +255,11 @@ def tile_scaleddotproductattention_t_kernel(tc, x, out):
                 scale_exp(b)
             if live(b + 1):
                 pe_scores(b + 1)
-            if live(b - 2):
-                finish(b - 2, banks)
             if live(b + 1):
                 act_ri(b + 1, rip)
             if live(b + 2):
                 act_xt(b + 2, xtp)
+            if live(b - 2):
+                finish(b - 2, banks)
             if live(b + LN):
                 sumsq(b + LN)

@@ -22,7 +22,7 @@ LX = 6
 LN = 4
 TAIL_A = 6
 TAIL_A2 = 3
-HEAD_V = 3
+HEAD_V = 0
 TAIL_V = 4
 LOAD_GROUPS = [1, 1, 2, 4, 4, 4, 4, 4, 4, 4]
 
@@ -108,7 +108,7 @@ def tile_scaleddotproductattention_t_kernel(tc, x, out):
             return rip
 
         def act_ri(b, rip):
-            ri = work3.tile([P, T * P], F32, name="RI")
+            ri = work2.tile([P, T * P], F32, name="RI")
             if b < HEAD_V or b >= B - TAIL_V:
                 nc.vector.tensor_copy(out=ri[:], in_=rip[:].rearrange("q t p -> q (t p)"))
             else:

@@ -22,8 +22,6 @@ LX = 6
 LN = 4
 TAIL_A = 6
 TAIL_A2 = 3
-HEAD_V = 0
-TAIL_V = 4
 LOAD_GROUPS = [1, 1, 2, 4, 4, 4, 4, 4, 4, 4]
 
 
@@ -37,8 +35,8 @@ def tile_scaleddotproductattention_t_kernel(tc, x, out):
         work5 = ctx.enter_context(tc.tile_pool(name="work5", bufs=10))
         work2 = ctx.enter_context(tc.tile_pool(name="work2", bufs=2))
         work3 = ctx.enter_context(tc.tile_pool(name="work3", bufs=3))
-        spool = ctx.enter_context(tc.tile_pool(name="spool", bufs=4))
-        gps = ctx.enter_context(tc.psum_pool(name="gps", bufs=4))
+        spool = ctx.enter_context(tc.tile_pool(name="spool", bufs=2))
+        gps = ctx.enter_context(tc.psum_pool(name="gps", bufs=1))
         tps = ctx.enter_context(tc.psum_pool(name="tps", bufs=1))
         ops = ctx.enter_context(tc.psum_pool(name="ops", bufs=1))
         if MANUAL:
@@ -71,6 +69,9 @@ def tile_scaleddotproductattention_t_kernel(tc, x, out):
         RI = {}
         xq = {}
         G = {}
+        S = {}
+        TB = {}
+        rm = {}
         E = {}
         rs = {}
         eq = {}
@@ -107,44 +108,80 @@ def tile_scaleddotproductattention_t_kernel(tc, x, out):
                 nc.tensor.transpose(rip[:, c, :], rn[b][:, c : c + 1].to_broadcast([P, P]), ident[:])
             return rip
 
-        def act_ri(b, rip):
+        def copy_ri(b, rip, on_vector):
             ri = work2.tile([P, T * P], F32, name="RI")
-            if b < HEAD_V or b >= B - TAIL_V:
+            if on_vector:
                 nc.vector.tensor_copy(out=ri[:], in_=rip[:].rearrange("q t p -> q (t p)"))
             else:
                 nc.scalar.copy(out=ri[:], in_=rip[:].rearrange("q t p -> q (t p)"))
             RI[b] = ri
 
-        def pe_scores(b):
+        def pe_scores(b, rows):
             xv = xT[b][:].bitcast(BF16).rearrange("q (n e) -> q n e", e=2)
-            G[b] = []
-            for t in range(T):
-                g = gps.tile([P, N], F32, name="g")
+            if rows[0] == 0:
+                ga = gps.tile([P, N], F32, name="ga")
+                G[b] = {0: ga[:]}
+                TB[b] = {}
+            elif rows[0] == 1:
+                gb = gps.tile([P, N], F32, name="gb")
+                G[b][1] = gb[:, 0 : 3 * P]
+                G[b][3] = gb[:, 3 * P : 4 * P]
+            else:
+                gc = gps.tile([P, N], F32, name="gc")
+                G[b][2] = gc[:, 0 : 2 * P]
+                TB[b][2] = gc[:, 2 * P : 4 * P]
+            for t in rows:
                 for e in range(2):
                     nc.tensor.matmul(
-                        g[:],
+                        G[b][t],
                         lhsT=xv[:, t * P : (t + 1) * P, e],
-                        rhs=xv[:, :, e],
+                        rhs=xv[:, t * P :, e],
                         start=(e == 0),
                         stop=(e == 1),
                     )
-                G[b].append(g)
 
-        def scale_exp(b):
+        def vec_scale(b):
+            S[b] = []
+            for t in range(T):
+                s = spool.tile([P, (T - t) * P], F32, name="s%d" % t)
+                nc.vector.scalar_tensor_tensor(
+                    out=s[:], in0=G[b][t], scalar=rn[b][:, t : t + 1], in1=RI[b][:, t * P :],
+                    op0=ALU.mult, op1=ALU.mult,
+                )
+                S[b].append(s)
+
+        def pe_mirror(b):
+            td = gps.tile([P, N], F32, name="td")
+            TB[b][1] = td[:, 0:P]
+            TB[b][3] = td[:, P:]
+            for t in range(T - 1):
+                for u in range(t + 1, T):
+                    nc.tensor.transpose(
+                        TB[b][u][:, t * P : (t + 1) * P], S[b][t][:, (u - t) * P : (u - t + 1) * P], ident[:]
+                    )
+
+        def exp_direct(b):
             et = work3.tile([P, T, N], BF16, name="E")
             r = small.tile([P, T], F32, name="rs")
             for t in range(T):
-                s = spool.tile([P, N], F32, name="s")
-                nc.vector.scalar_tensor_tensor(
-                    out=s[:], in0=G[b][t][:], scalar=rn[b][:, t : t + 1], in1=RI[b][:],
-                    op0=ALU.mult, op1=ALU.mult,
-                )
                 nc.scalar.activation(
-                    out=et[:, t, :], in_=s[:], func=ACTF.Exp, bias=-1.0, scale=1.0,
+                    out=et[:, t, t * P :], in_=S[b][t][:], func=ACTF.Exp, bias=-1.0, scale=1.0,
                     accum_out=r[:, t : t + 1],
                 )
             E[b] = et
             rs[b] = r
+
+        def exp_mirror(b):
+            r = small.tile([P, T - 1], F32, name="rm")
+            for t in (2, 1, 3):
+                nc.scalar.activation(
+                    out=E[b][:, t, : t * P], in_=TB[b][t], func=ACTF.Exp, bias=-1.0, scale=1.0,
+                    accum_out=r[:, t - 1 : t],
+                )
+            rm[b] = r
+
+        def add_sums(b):
+            nc.gpsimd.tensor_tensor(out=rs[b][:, 1:], in0=rs[b][:, 1:], in1=rm[b][:], op=ALU.add)
 
         def x_regroup(b):
             xg = work2.tile([P, D, T], BF16, name="xg", align_bytes=64)
@@ -249,14 +286,24 @@ def tile_scaleddotproductattention_t_kernel(tc, x, out):
                 banks = pe_mx(b - 2)
             if live(b - 1):
                 egs[b - 1] = e_regroup(b - 1, b - 1 == B - 1)
+                add_sums(b - 1)
             if live(b + LN - 1):
                 rsqrt(b + LN - 1)
             if live(b):
-                scale_exp(b)
+                vec_scale(b)
             if live(b + 1):
-                pe_scores(b + 1)
+                pe_scores(b + 1, [0])
+            if live(b):
+                pe_mirror(b)
+                exp_direct(b)
             if live(b + 1):
-                act_ri(b + 1, rip)
+                pe_scores(b + 1, [1, 3])
+            if live(b):
+                exp_mirror(b)
+            if live(b + 1):
+                pe_scores(b + 1, [2])
+            if live(b + 1):
+                copy_ri(b + 1, rip, (b + 1) % 2 == 1)
             if live(b + 2):
                 act_xt(b + 2, xtp)
             if live(b - 2):

@@ -19,10 +19,12 @@ T = N // P
 FLOPS = 2 * (2 * B * N * N * D)
 MANUAL = True
 LX = 6
-LN = 4
+LN = 6
+LN0 = 4
 TAIL_A = 6
 TAIL_A2 = 3
 LOAD_GROUPS = [1, 1, 2, 4, 4, 4, 4, 4, 4, 4]
+NORM_GROUPS = [(g, k, nb) for g, nb in enumerate(LOAD_GROUPS) for k in range(nb)]
 
 
 def tile_scaleddotproductattention_t_kernel(tc, x, out):
@@ -30,6 +32,7 @@ def tile_scaleddotproductattention_t_kernel(tc, x, out):
     with ExitStack() as ctx:
         const = ctx.enter_context(tc.tile_pool(name="const", bufs=1))
         xres = ctx.enter_context(tc.tile_pool(name="xres", bufs=1))
+        norms = ctx.enter_context(tc.tile_pool(name="norms", bufs=1))
         small = ctx.enter_context(tc.tile_pool(name="small", bufs=8))
         one = ctx.enter_context(tc.tile_pool(name="one", bufs=1))
         work5 = ctx.enter_context(tc.tile_pool(name="work5", bufs=10))
@@ -60,7 +63,7 @@ def tile_scaleddotproductattention_t_kernel(tc, x, out):
 
         ident = const.tile([P, P], F32, name="ident")
         make_identity(nc, ident[:])
-        mhalf = const.tile([P, T], F32, name="mhalf")
+        mhalf = const.tile([P, 4 * T], F32, name="mhalf")
         nc.vector.memset(mhalf[:], -0.5)
 
         rn = {}
@@ -78,18 +81,24 @@ def tile_scaleddotproductattention_t_kernel(tc, x, out):
         rinv = {}
 
         def sumsq(b):
-            q = small.tile([P, T], F32, name="nsq")
+            g, k, nb = NORM_GROUPS[b]
+            if k == 0:
+                nsq[g] = norms.tile([P, nb * T], F32, name="nsq%d" % g)
+            q = nsq[g][:, k * T : (k + 1) * T]
             for t in range(T):
                 junk = work2.tile([P, D], BF16, name="junk")
                 nc.scalar.activation(
                     out=junk[:], in_=xb3[b][:, t, :], func=ACTF.Square, accum_out=q[:, t : t + 1]
                 )
-            nsq[b] = q
 
         def rsqrt(b):
-            r = small.tile([P, T], F32, name="rn")
-            nc.gpsimd.tensor_tensor(out=r[:], in0=nsq[b][:], in1=mhalf[:], op=ALU.pow)
-            rn[b] = r
+            g, k, nb = NORM_GROUPS[b]
+            if k < nb - 1:
+                return
+            r = norms.tile([P, nb * T], F32, name="rn%d" % g)
+            nc.gpsimd.tensor_tensor(out=r[:], in0=nsq[g][:], in1=mhalf[:, : nb * T], op=ALU.pow)
+            for j in range(nb):
+                rn[b - nb + 1 + j] = r[:, j * T : (j + 1) * T]
 
         def pe_xt(b):
             xtp = tps.tile([P, T, P], F32, name="xtp")
@@ -181,7 +190,7 @@ def tile_scaleddotproductattention_t_kernel(tc, x, out):
             rm[b] = r
 
         def add_sums(b):
-            nc.gpsimd.tensor_tensor(out=rs[b][:, 1:], in0=rs[b][:, 1:], in1=rm[b][:], op=ALU.add)
+            nc.vector.tensor_tensor(out=rs[b][:, 1:], in0=rs[b][:, 1:], in1=rm[b][:], op=ALU.add)
 
         def x_regroup(b):
             xg = work2.tile([P, D, T], BF16, name="xg", align_bytes=64)
@@ -270,7 +279,16 @@ def tile_scaleddotproductattention_t_kernel(tc, x, out):
                     )
             nc.sync.dma_start(out=out[bb].rearrange("(r c) d -> r c d", c=T), in_=o[:])
 
-        for b in range(-max(LX, LN), B + 2):
+        def squared(b):
+            if b < 0:
+                return [b + LN0] if b + LN0 >= 0 else []
+            if b < 2:
+                return [2 * b + LN0, 2 * b + LN0 + 1]
+            return [b + LN] if b + LN < B else []
+
+        for b in range(-LX, B + 2):
+            if live(b - 2):
+                add_sums(b - 2)
             if live(b + LX):
                 xgs[b + LX] = x_regroup(b + LX)
             if live(b + LX - 1):
@@ -286,9 +304,8 @@ def tile_scaleddotproductattention_t_kernel(tc, x, out):
                 banks = pe_mx(b - 2)
             if live(b - 1):
                 egs[b - 1] = e_regroup(b - 1, b - 1 == B - 1)
-                add_sums(b - 1)
-            if live(b + LN - 1):
-                rsqrt(b + LN - 1)
+            for n in squared(b - 1):
+                rsqrt(n)
             if live(b):
                 vec_scale(b)
             if live(b + 1):
@@ -308,5 +325,5 @@ def tile_scaleddotproductattention_t_kernel(tc, x, out):
                 act_xt(b + 2, xtp)
             if live(b - 2):
                 finish(b - 2, banks)
-            if live(b + LN):
-                sumsq(b + LN)
+            for n in squared(b):
+                sumsq(n)

@@ -9,6 +9,7 @@ F32 = mybir.dt.float32
 BF16 = mybir.dt.bfloat16
 U32 = mybir.dt.uint32
 U8 = mybir.dt.uint8
+I32 = mybir.dt.int32
 FP8X4 = mybir.dt.float8_e4m3fn_x4
 ALU = mybir.AluOpType
 ACTF = mybir.ActivationFunctionType
@@ -19,12 +20,14 @@ T = N // P
 FLOPS = 2 * (2 * B * N * N * D)
 MANUAL = True
 LX = 6
-LN = 6
+LN = 8
 LN0 = 4
+SEED = 1597463007.0
 TAIL_A = 6
 TAIL_A2 = 3
 LOAD_GROUPS = [1, 1, 2, 4, 4, 4, 4, 4, 4, 4]
-NORM_GROUPS = [(g, k, nb) for g, nb in enumerate(LOAD_GROUPS) for k in range(nb)]
+NORM_GROUPS = [(g, k, nb) for g, nb in enumerate([1, 1, 2, 2, 2, 4, 4, 4, 4, 4, 4]) for k in range(nb)]
+POW_GROUPS = 5
 
 
 def tile_scaleddotproductattention_t_kernel(tc, x, out):
@@ -32,6 +35,7 @@ def tile_scaleddotproductattention_t_kernel(tc, x, out):
     with ExitStack() as ctx:
         const = ctx.enter_context(tc.tile_pool(name="const", bufs=1))
         xres = ctx.enter_context(tc.tile_pool(name="xres", bufs=1))
+        newt = ctx.enter_context(tc.tile_pool(name="newt", bufs=2))
         norms = ctx.enter_context(tc.tile_pool(name="norms", bufs=1))
         small = ctx.enter_context(tc.tile_pool(name="small", bufs=8))
         one = ctx.enter_context(tc.tile_pool(name="one", bufs=1))
@@ -63,7 +67,7 @@ def tile_scaleddotproductattention_t_kernel(tc, x, out):
 
         ident = const.tile([P, P], F32, name="ident")
         make_identity(nc, ident[:])
-        mhalf = const.tile([P, 4 * T], F32, name="mhalf")
+        mhalf = const.tile([P, 2 * T], F32, name="mhalf")
         nc.vector.memset(mhalf[:], -0.5)
 
         rn = {}
@@ -75,6 +79,9 @@ def tile_scaleddotproductattention_t_kernel(tc, x, out):
         S = {}
         TB = {}
         rm = {}
+        chores = []
+        guess = {}
+        part = {}
         E = {}
         rs = {}
         eq = {}
@@ -93,12 +100,53 @@ def tile_scaleddotproductattention_t_kernel(tc, x, out):
 
         def rsqrt(b):
             g, k, nb = NORM_GROUPS[b]
-            if k < nb - 1:
-                return
-            r = norms.tile([P, nb * T], F32, name="rn%d" % g)
-            nc.gpsimd.tensor_tensor(out=r[:], in0=nsq[g][:], in1=mhalf[:, : nb * T], op=ALU.pow)
+            if k == nb - 1 and g < POW_GROUPS:
+                r = norms.tile([P, nb * T], F32, name="rn%d" % g)
+                nc.gpsimd.tensor_tensor(out=r[:], in0=nsq[g][:], in1=mhalf[:, : nb * T], op=ALU.pow)
+                set_rn(b, r[:])
+
+        def queue_newton(b):
+            g, k, nb = NORM_GROUPS[b]
+            if k == nb - 1 and g >= POW_GROUPS:
+                chores.extend([lambda step=step: newton(b, step) for step in range(10)])
+
+        def set_rn(b, r):
+            g, k, nb = NORM_GROUPS[b]
             for j in range(nb):
                 rn[b - nb + 1 + j] = r[:, j * T : (j + 1) * T]
+
+        def newton(b, step):
+            g, k, nb = NORM_GROUPS[b]
+            q = nsq[g]
+            if step == 0:
+                y0 = newt.tile([P, nb * T], I32, name="y0")
+                nc.vector.tensor_scalar(
+                    out=y0[:], in0=q[:].bitcast(I32), scalar1=-0.5, scalar2=SEED, op0=ALU.mult, op1=ALU.add
+                )
+                guess[g] = y0[:].bitcast(F32)
+            elif step % 3 == 1:
+                u = newt.tile([P, nb * T], F32, name="u")
+                nc.vector.scalar_tensor_tensor(
+                    out=u[:], in0=guess[g], scalar=-0.5, in1=guess[g], op0=ALU.mult, op1=ALU.mult
+                )
+                part[g] = u[:]
+            elif step % 3 == 2:
+                w = newt.tile([P, nb * T], F32, name="w")
+                nc.vector.tensor_tensor(out=w[:], in0=part[g], in1=q[:], op=ALU.mult)
+                part[g] = w[:]
+            else:
+                y = norms.tile([P, nb * T], F32, name="y%d_%d" % (g, step))
+                nc.vector.scalar_tensor_tensor(
+                    out=y[:], in0=part[g], scalar=1.5, in1=guess[g], op0=ALU.add, op1=ALU.mult
+                )
+                guess[g] = y[:]
+                if step == 9:
+                    set_rn(b, y[:])
+
+        def chore():
+            if chores:
+                chores[0]()
+                chores.remove(chores[0])
 
         def pe_xt(b):
             xtp = tps.tile([P, T, P], F32, name="xtp")
@@ -282,17 +330,22 @@ def tile_scaleddotproductattention_t_kernel(tc, x, out):
         def squared(b):
             if b < 0:
                 return [b + LN0] if b + LN0 >= 0 else []
-            if b < 2:
+            if b < 4:
                 return [2 * b + LN0, 2 * b + LN0 + 1]
             return [b + LN] if b + LN < B else []
 
         for b in range(-LX, B + 2):
+            for n in squared(b - 1):
+                queue_newton(n)
             if live(b - 2):
                 add_sums(b - 2)
+            chore()
             if live(b + LX):
                 xgs[b + LX] = x_regroup(b + LX)
+            chore()
             if live(b + LX - 1):
                 x_quant(b + LX - 1, xgs[b + LX - 1])
+            chore()
             if live(b - 2):
                 recip(b - 2)
                 e_quant(b - 2, egs[b - 2])
@@ -320,7 +373,7 @@ def tile_scaleddotproductattention_t_kernel(tc, x, out):
             if live(b + 1):
                 pe_scores(b + 1, [2])
             if live(b + 1):
-                copy_ri(b + 1, rip, (b + 1) % 2 == 1)
+                copy_ri(b + 1, rip, (b + 1) % 3 == 1)
             if live(b + 2):
                 act_xt(b + 2, xtp)
             if live(b - 2):

@@ -8,8 +8,8 @@ from concourse.masks import make_identity
 F32 = mybir.dt.float32
 BF16 = mybir.dt.bfloat16
 U32 = mybir.dt.uint32
-U8 = mybir.dt.uint8
 I32 = mybir.dt.int32
+U8 = mybir.dt.uint8
 FP8X4 = mybir.dt.float8_e4m3fn_x4
 ALU = mybir.AluOpType
 ACTF = mybir.ActivationFunctionType
@@ -18,16 +18,19 @@ P = 128
 B, N, D = 32, 512, 256
 T = N // P
 FLOPS = 2 * (2 * B * N * N * D)
-MANUAL = True
-LX = 6
-LN = 8
-LN0 = 4
+LD = 12
+LB = 13
+LX = 12
+LR = 2
+SQ_S = 12
+XT_V = 6
+NG = 4
 SEED = 1597463007.0
-TAIL_A = 6
-TAIL_A2 = 3
 LOAD_GROUPS = [1, 1, 2, 4, 4, 4, 4, 4, 4, 4]
-NORM_GROUPS = [(g, k, nb) for g, nb in enumerate([1, 1, 2, 2, 2, 4, 4, 4, 4, 4, 4]) for k in range(nb)]
-POW_GROUPS = 5
+
+
+def fin_on_scalar(b, h):
+    return b < B - 12 or (h == 0 and b % 2 == 1)
 
 
 def tile_scaleddotproductattention_t_kernel(tc, x, out):
@@ -39,15 +42,12 @@ def tile_scaleddotproductattention_t_kernel(tc, x, out):
         norms = ctx.enter_context(tc.tile_pool(name="norms", bufs=1))
         small = ctx.enter_context(tc.tile_pool(name="small", bufs=8))
         one = ctx.enter_context(tc.tile_pool(name="one", bufs=1))
-        work5 = ctx.enter_context(tc.tile_pool(name="work5", bufs=10))
+        deep = ctx.enter_context(tc.tile_pool(name="deep", bufs=15))
         work2 = ctx.enter_context(tc.tile_pool(name="work2", bufs=2))
         work3 = ctx.enter_context(tc.tile_pool(name="work3", bufs=3))
-        spool = ctx.enter_context(tc.tile_pool(name="spool", bufs=2))
+        work4 = ctx.enter_context(tc.tile_pool(name="work4", bufs=4))
         gps = ctx.enter_context(tc.psum_pool(name="gps", bufs=1))
-        tps = ctx.enter_context(tc.psum_pool(name="tps", bufs=1))
-        ops = ctx.enter_context(tc.psum_pool(name="ops", bufs=1))
-        if MANUAL:
-            ctx.enter_context(tc.manual_schedule())
+        ctx.enter_context(tc.manual_schedule())
 
         xb3 = []
         xbw = []
@@ -67,10 +67,10 @@ def tile_scaleddotproductattention_t_kernel(tc, x, out):
 
         ident = const.tile([P, P], F32, name="ident")
         make_identity(nc, ident[:])
-        mhalf = const.tile([P, 2 * T], F32, name="mhalf")
-        nc.vector.memset(mhalf[:], -0.5)
+        rna = const.tile([P, B * T], F32, name="rna")
+        nc.vector.memset(rna[:], 1.0)
+        park = out[B - 1].rearrange("n d -> (n d)")
 
-        rn = {}
         nsq = {}
         xT = {}
         RI = {}
@@ -79,99 +79,122 @@ def tile_scaleddotproductattention_t_kernel(tc, x, out):
         S = {}
         TB = {}
         rm = {}
-        chores = []
-        guess = {}
-        part = {}
         E = {}
         rs = {}
         eq = {}
         rinv = {}
+        chores = []
+        guess = {}
+        part = {}
+
+        def nsq_cols(b):
+            g, k = divmod(b, NG)
+            if k == 0:
+                nsq[g] = norms.tile([P, NG * T], F32, name="nsq%d" % g)
+            return nsq[g][:, k * T : (k + 1) * T]
 
         def sumsq(b):
-            g, k, nb = NORM_GROUPS[b]
-            if k == 0:
-                nsq[g] = norms.tile([P, nb * T], F32, name="nsq%d" % g)
-            q = nsq[g][:, k * T : (k + 1) * T]
+            q = nsq_cols(b)
             for t in range(T):
                 junk = work2.tile([P, D], BF16, name="junk")
                 nc.scalar.activation(
                     out=junk[:], in_=xb3[b][:, t, :], func=ACTF.Square, accum_out=q[:, t : t + 1]
                 )
 
-        def rsqrt(b):
-            g, k, nb = NORM_GROUPS[b]
-            if k == nb - 1 and g < POW_GROUPS:
-                r = norms.tile([P, nb * T], F32, name="rn%d" % g)
-                nc.gpsimd.tensor_tensor(out=r[:], in0=nsq[g][:], in1=mhalf[:, : nb * T], op=ALU.pow)
-                set_rn(b, r[:])
+        def pe_diag(b):
+            xv = xT[b][:].bitcast(BF16).rearrange("q (n e) -> q n e", e=2)
+            dg = gps.tile([P, T, P], F32, name="dg")
+            for t in range(T):
+                for e in range(2):
+                    nc.tensor.matmul(
+                        dg[:, t, :],
+                        lhsT=xv[:, t * P : (t + 1) * P, e],
+                        rhs=xv[:, t * P : (t + 1) * P, e],
+                        start=(e == 0),
+                        stop=(e == 1),
+                    )
+            return dg
 
-        def queue_newton(b):
-            g, k, nb = NORM_GROUPS[b]
-            if k == nb - 1 and g >= POW_GROUPS:
-                chores.extend([lambda step=step: newton(b, step) for step in range(10)])
+        def vec_diag(b, dg):
+            q = nsq_cols(b)
+            for t in range(T):
+                junk = work2.tile([P, P], BF16, name="djunk")
+                nc.vector.scalar_tensor_tensor(
+                    out=junk[:], in0=dg[:, t, :], scalar=1.0, in1=ident[:],
+                    op0=ALU.mult, op1=ALU.mult, accum_out=q[:, t : t + 1],
+                )
 
-        def set_rn(b, r):
-            g, k, nb = NORM_GROUPS[b]
-            for j in range(nb):
-                rn[b - nb + 1 + j] = r[:, j * T : (j + 1) * T]
-
-        def newton(b, step):
-            g, k, nb = NORM_GROUPS[b]
+        def newton(g, step):
             q = nsq[g]
             if step == 0:
-                y0 = newt.tile([P, nb * T], I32, name="y0")
+                y0 = newt.tile([P, NG * T], I32, name="y0")
                 nc.vector.tensor_scalar(
                     out=y0[:], in0=q[:].bitcast(I32), scalar1=-0.5, scalar2=SEED, op0=ALU.mult, op1=ALU.add
                 )
                 guess[g] = y0[:].bitcast(F32)
             elif step % 3 == 1:
-                u = newt.tile([P, nb * T], F32, name="u")
+                u = newt.tile([P, NG * T], F32, name="u")
                 nc.vector.scalar_tensor_tensor(
                     out=u[:], in0=guess[g], scalar=-0.5, in1=guess[g], op0=ALU.mult, op1=ALU.mult
                 )
                 part[g] = u[:]
             elif step % 3 == 2:
-                w = newt.tile([P, nb * T], F32, name="w")
+                w = newt.tile([P, NG * T], F32, name="w")
                 nc.vector.tensor_tensor(out=w[:], in0=part[g], in1=q[:], op=ALU.mult)
                 part[g] = w[:]
             else:
-                y = norms.tile([P, nb * T], F32, name="y%d_%d" % (g, step))
+                if step < 9:
+                    y = newt.tile([P, NG * T], F32, name="y%d" % step)
+                    y = y[:]
+                else:
+                    y = rna[:, g * NG * T : (g + 1) * NG * T]
                 nc.vector.scalar_tensor_tensor(
-                    out=y[:], in0=part[g], scalar=1.5, in1=guess[g], op0=ALU.add, op1=ALU.mult
+                    out=y, in0=part[g], scalar=1.5, in1=guess[g], op0=ALU.add, op1=ALU.mult
                 )
-                guess[g] = y[:]
-                if step == 9:
-                    set_rn(b, y[:])
+                guess[g] = y
+
+        def pe_rows(g):
+            rows = gps.tile([P, P], F32, name="dg")
+            nc.tensor.transpose(rows[:], rna[:], ident[:])
+            part[g] = rows
+
+        def park_rows(g):
+            rt = work2.tile([P, P], F32, name="rt")
+            nc.vector.tensor_copy(out=rt[:], in_=part[g][:])
+            r0, r1 = g * NG * T, (g + 1) * NG * T
+            nc.sync.dma_start(
+                out=park[r0 * P : r1 * P].rearrange("(r p) -> r p", p=P), in_=rt[r0:r1, :]
+            )
+
+        def queue_norms(b):
+            g, k = divmod(b, NG)
+            if k == NG - 1:
+                chores.extend([lambda step=step: newton(g, step) for step in range(10)])
+                chores.extend([lambda: pe_rows(g), lambda: park_rows(g)])
 
         def chore():
             if chores:
                 chores[0]()
                 chores.remove(chores[0])
 
+        def load_ri(b):
+            ri = work4.tile([P, N], F32, name="RI")
+            nc.sync.dma_start(out=ri[:], in_=park[b * N : (b + 1) * N].partition_broadcast(P))
+            RI[b] = ri
+
         def pe_xt(b):
-            xtp = tps.tile([P, T, P], F32, name="xtp")
+            xtp = gps.tile([P, T, P], F32, name="xtp")
             for t in range(T):
                 nc.tensor.transpose(xtp[:, t, :], xbw[b][:, t * P : (t + 1) * P], ident[:])
             return xtp
 
-        def act_xt(b, xtp):
-            xs = work3.tile([P, T * P], F32, name="xT")
-            nc.scalar.copy(out=xs[:], in_=xtp[:].rearrange("q t p -> q (t p)"))
-            xT[b] = xs
-
-        def pe_ri(b):
-            rip = tps.tile([P, T, P], F32, name="rip")
-            for c in range(T):
-                nc.tensor.transpose(rip[:, c, :], rn[b][:, c : c + 1].to_broadcast([P, P]), ident[:])
-            return rip
-
-        def copy_ri(b, rip, on_vector):
-            ri = work2.tile([P, T * P], F32, name="RI")
-            if on_vector:
-                nc.vector.tensor_copy(out=ri[:], in_=rip[:].rearrange("q t p -> q (t p)"))
+        def copy_xt(b, xtp):
+            xs = deep.tile([P, T * P], F32, name="xT")
+            if b < XT_V:
+                nc.vector.tensor_copy(out=xs[:], in_=xtp[:].rearrange("q t p -> q (t p)"))
             else:
-                nc.scalar.copy(out=ri[:], in_=rip[:].rearrange("q t p -> q (t p)"))
-            RI[b] = ri
+                nc.scalar.copy(out=xs[:], in_=xtp[:].rearrange("q t p -> q (t p)"))
+            xT[b] = xs
 
         def pe_scores(b, rows):
             xv = xT[b][:].bitcast(BF16).rearrange("q (n e) -> q n e", e=2)
@@ -200,9 +223,9 @@ def tile_scaleddotproductattention_t_kernel(tc, x, out):
         def vec_scale(b):
             S[b] = []
             for t in range(T):
-                s = spool.tile([P, (T - t) * P], F32, name="s%d" % t)
+                s = work2.tile([P, (T - t) * P], F32, name="s%d" % t)
                 nc.vector.scalar_tensor_tensor(
-                    out=s[:], in0=G[b][t], scalar=rn[b][:, t : t + 1], in1=RI[b][:, t * P :],
+                    out=s[:], in0=G[b][t], scalar=rna[:, b * T + t : b * T + t + 1], in1=RI[b][:, t * P :],
                     op0=ALU.mult, op1=ALU.mult,
                 )
                 S[b].append(s)
@@ -249,8 +272,8 @@ def tile_scaleddotproductattention_t_kernel(tc, x, out):
             return xg
 
         def x_quant(b, xg):
-            w = work5.tile([P, D], U32, name="xq", align_bytes=64)
-            sc = work5.tile([P, D], U8, name="xsc", align_bytes=64)
+            w = deep.tile([P, D], U32, name="xq", align_bytes=64)
+            sc = deep.tile([P, D], U8, name="xsc", align_bytes=64)
             nc.vector.quantize_mx(
                 out=w[:].bitcast(FP8X4), scales=sc[:], in_=xg[:].rearrange("p d t -> p (d t)")
             )
@@ -288,7 +311,7 @@ def tile_scaleddotproductattention_t_kernel(tc, x, out):
             xw, xsc = xq[b]
             banks = []
             for h in range(2):
-                o = ops.tile([P, 2, D], F32, name="op%d" % h)
+                o = gps.tile([P, 2, D], F32, name="op%d" % h)
                 for k in range(2):
                     c = 2 * h + k
                     nc.tensor.matmul_mx(
@@ -309,34 +332,27 @@ def tile_scaleddotproductattention_t_kernel(tc, x, out):
         def live(b):
             return 0 <= b < B
 
-        def finish(bb, banks):
+        def finish(b, banks):
             o = work3.tile([P, T, D], F32, name="o")
             for h in range(2):
-                if bb >= B - (TAIL_A if h == 0 else TAIL_A2):
+                if fin_on_scalar(b, h):
                     for k in range(2):
                         c = 2 * h + k
                         nc.scalar.activation(
                             out=o[:, c, :], in_=banks[h][:, k, :], func=ACTF.Copy,
-                            scale=rinv[bb][:, c : c + 1],
+                            scale=rinv[b][:, c : c + 1],
                         )
                 else:
                     nc.vector.tensor_tensor(
                         out=o[:, 2 * h : 2 * h + 2, :], in0=banks[h][:],
-                        in1=rinv[bb][:, 2 * h : 2 * h + 2].unsqueeze(2).to_broadcast([P, 2, D]),
+                        in1=rinv[b][:, 2 * h : 2 * h + 2].unsqueeze(2).to_broadcast([P, 2, D]),
                         op=ALU.mult,
                     )
-            nc.sync.dma_start(out=out[bb].rearrange("(r c) d -> r c d", c=T), in_=o[:])
+            nc.sync.dma_start(out=out[b].rearrange("(r c) d -> r c d", c=T), in_=o[:])
 
-        def squared(b):
-            if b < 0:
-                return [b + LN0] if b + LN0 >= 0 else []
-            if b < 4:
-                return [2 * b + LN0, 2 * b + LN0 + 1]
-            return [b + LN] if b + LN < B else []
-
-        for b in range(-LX, B + 2):
-            for n in squared(b - 1):
-                queue_newton(n)
+        for b in range(-LB, B + 2):
+            if live(b + LD - 2):
+                queue_norms(b + LD - 2)
             if live(b - 2):
                 add_sums(b - 2)
             chore()
@@ -346,19 +362,19 @@ def tile_scaleddotproductattention_t_kernel(tc, x, out):
             if live(b + LX - 1):
                 x_quant(b + LX - 1, xgs[b + LX - 1])
             chore()
+            if live(b + LR):
+                load_ri(b + LR)
             if live(b - 2):
                 recip(b - 2)
                 e_quant(b - 2, egs[b - 2])
-            if live(b + 2):
-                xtp = pe_xt(b + 2)
-            if live(b + 1):
-                rip = pe_ri(b + 1)
+            if live(b + LB):
+                xtp = pe_xt(b + LB)
+            if live(b + LD) and b + LD >= SQ_S:
+                dg = pe_diag(b + LD)
             if live(b - 2):
                 banks = pe_mx(b - 2)
             if live(b - 1):
                 egs[b - 1] = e_regroup(b - 1, b - 1 == B - 1)
-            for n in squared(b - 1):
-                rsqrt(n)
             if live(b):
                 vec_scale(b)
             if live(b + 1):
@@ -372,11 +388,12 @@ def tile_scaleddotproductattention_t_kernel(tc, x, out):
                 exp_mirror(b)
             if live(b + 1):
                 pe_scores(b + 1, [2])
-            if live(b + 1):
-                copy_ri(b + 1, rip, (b + 1) % 3 == 1)
-            if live(b + 2):
-                act_xt(b + 2, xtp)
+            if live(b + LB):
+                copy_xt(b + LB, xtp)
+            if live(b + LD):
+                if b + LD < SQ_S:
+                    sumsq(b + LD)
+                else:
+                    vec_diag(b + LD, dg)
             if live(b - 2):
                 finish(b - 2, banks)
-            for n in squared(b):
-                sumsq(n)

@@ -18,19 +18,37 @@ P = 128
 B, N, D = 32, 512, 256
 T = N // P
 FLOPS = 2 * (2 * B * N * N * D)
-LD = 12
-LB = 13
-LX = 12
-LR = 2
-SQ_S = 12
-XT_V = 6
-NG = 4
+LD0 = 10
+LB = 3
+LX = 10
+LR = 1
+XT_V = 0
+GROUPS = [2, 5, 5, 7, 9, 4]
+GROUP_OF = [(g, k) for g, nb in enumerate(GROUPS) for k in range(nb)]
+FIRST = [sum(GROUPS[:g]) for g in range(len(GROUPS))]
+TAIL = B - 12
+PAIRS = B - 12
+DUMMIES = 1
 SEED = 1597463007.0
 LOAD_GROUPS = [1, 1, 2, 4, 4, 4, 4, 4, 4, 4]
+EARLY = 5
+LOAD_AT = [-5, -2, 0, 2, 5]
 
 
 def fin_on_scalar(b, h):
-    return b < B - 12 or (h == 0 and b % 2 == 1)
+    return h == 0 and b >= TAIL
+
+
+def regroup_on_vector(b):
+    return b == B - 1
+
+
+def squared_by(b):
+    return max(0, min(B, b + LD0 + 1 + max(0, (b + 1) // 3)))
+
+
+def squared(b):
+    return range(squared_by(b - 1), squared_by(b))
 
 
 def tile_scaleddotproductattention_t_kernel(tc, x, out):
@@ -51,8 +69,9 @@ def tile_scaleddotproductattention_t_kernel(tc, x, out):
 
         xb3 = []
         xbw = []
-        b0 = 0
-        for g, nb in enumerate(LOAD_GROUPS):
+        def load_x(g):
+            nb = LOAD_GROUPS[g]
+            b0 = sum(LOAD_GROUPS[:g])
             xt = xres.tile([P, nb * T * D], BF16, name="x%d" % g)
             nc.sync.dma_start(
                 out=xt[:].rearrange("p (k n) -> p k n", n=T * D),
@@ -63,10 +82,14 @@ def tile_scaleddotproductattention_t_kernel(tc, x, out):
             for k in range(nb):
                 xb3.append(v3[:, k])
                 xbw.append(vw[:, k * (T * D // 2) : (k + 1) * (T * D // 2)])
-            b0 += nb
+
+        for g in range(EARLY):
+            load_x(g)
 
         ident = const.tile([P, P], F32, name="ident")
         make_identity(nc, ident[:])
+        mhalf = const.tile([P, GROUPS[0] * T], F32, name="mhalf")
+        nc.vector.memset(mhalf[:], -0.5)
         rna = const.tile([P, B * T], F32, name="rna")
         nc.vector.memset(rna[:], 1.0)
         park = out[B - 1].rearrange("n d -> (n d)")
@@ -84,13 +107,14 @@ def tile_scaleddotproductattention_t_kernel(tc, x, out):
         eq = {}
         rinv = {}
         chores = []
+        parked = []
         guess = {}
         part = {}
 
         def nsq_cols(b):
-            g, k = divmod(b, NG)
+            g, k = GROUP_OF[b]
             if k == 0:
-                nsq[g] = norms.tile([P, NG * T], F32, name="nsq%d" % g)
+                nsq[g] = norms.tile([P, GROUPS[g] * T], F32, name="nsq%d" % g)
             return nsq[g][:, k * T : (k + 1) * T]
 
         def sumsq(b):
@@ -101,53 +125,31 @@ def tile_scaleddotproductattention_t_kernel(tc, x, out):
                     out=junk[:], in_=xb3[b][:, t, :], func=ACTF.Square, accum_out=q[:, t : t + 1]
                 )
 
-        def pe_diag(b):
-            xv = xT[b][:].bitcast(BF16).rearrange("q (n e) -> q n e", e=2)
-            dg = gps.tile([P, T, P], F32, name="dg")
-            for t in range(T):
-                for e in range(2):
-                    nc.tensor.matmul(
-                        dg[:, t, :],
-                        lhsT=xv[:, t * P : (t + 1) * P, e],
-                        rhs=xv[:, t * P : (t + 1) * P, e],
-                        start=(e == 0),
-                        stop=(e == 1),
-                    )
-            return dg
-
-        def vec_diag(b, dg):
-            q = nsq_cols(b)
-            for t in range(T):
-                junk = work2.tile([P, P], BF16, name="djunk")
-                nc.vector.scalar_tensor_tensor(
-                    out=junk[:], in0=dg[:, t, :], scalar=1.0, in1=ident[:],
-                    op0=ALU.mult, op1=ALU.mult, accum_out=q[:, t : t + 1],
-                )
-
         def newton(g, step):
             q = nsq[g]
+            w = GROUPS[g] * T
             if step == 0:
-                y0 = newt.tile([P, NG * T], I32, name="y0")
+                y0 = newt.tile([P, w], I32, name="y0")
                 nc.vector.tensor_scalar(
                     out=y0[:], in0=q[:].bitcast(I32), scalar1=-0.5, scalar2=SEED, op0=ALU.mult, op1=ALU.add
                 )
                 guess[g] = y0[:].bitcast(F32)
             elif step % 3 == 1:
-                u = newt.tile([P, NG * T], F32, name="u")
+                u = newt.tile([P, w], F32, name="u")
                 nc.vector.scalar_tensor_tensor(
                     out=u[:], in0=guess[g], scalar=-0.5, in1=guess[g], op0=ALU.mult, op1=ALU.mult
                 )
                 part[g] = u[:]
             elif step % 3 == 2:
-                w = newt.tile([P, NG * T], F32, name="w")
-                nc.vector.tensor_tensor(out=w[:], in0=part[g], in1=q[:], op=ALU.mult)
-                part[g] = w[:]
+                v = newt.tile([P, w], F32, name="v")
+                nc.vector.tensor_tensor(out=v[:], in0=part[g], in1=q[:], op=ALU.mult)
+                part[g] = v[:]
             else:
                 if step < 9:
-                    y = newt.tile([P, NG * T], F32, name="y%d" % step)
+                    y = newt.tile([P, w], F32, name="y%d" % step)
                     y = y[:]
                 else:
-                    y = rna[:, g * NG * T : (g + 1) * NG * T]
+                    y = rna[:, FIRST[g] * T : FIRST[g] * T + w]
                 nc.vector.scalar_tensor_tensor(
                     out=y, in0=part[g], scalar=1.5, in1=guess[g], op0=ALU.add, op1=ALU.mult
                 )
@@ -159,17 +161,27 @@ def tile_scaleddotproductattention_t_kernel(tc, x, out):
             part[g] = rows
 
         def park_rows(g):
+            parked.append(g)
             rt = work2.tile([P, P], F32, name="rt")
             nc.vector.tensor_copy(out=rt[:], in_=part[g][:])
-            r0, r1 = g * NG * T, (g + 1) * NG * T
+            r0, r1 = FIRST[g] * T, (FIRST[g] + GROUPS[g]) * T
             nc.sync.dma_start(
                 out=park[r0 * P : r1 * P].rearrange("(r p) -> r p", p=P), in_=rt[r0:r1, :]
             )
 
+        def power(g):
+            w = GROUPS[g] * T
+            nc.gpsimd.tensor_tensor(
+                out=rna[:, FIRST[g] * T : FIRST[g] * T + w], in0=nsq[g][:], in1=mhalf[:, :w], op=ALU.pow
+            )
+
         def queue_norms(b):
-            g, k = divmod(b, NG)
-            if k == NG - 1:
-                chores.extend([lambda step=step: newton(g, step) for step in range(10)])
+            g, k = GROUP_OF[b]
+            if k == GROUPS[g] - 1:
+                if g == 0:
+                    power(g)
+                else:
+                    chores.extend([lambda step=step: newton(g, step) for step in range(10)])
                 chores.extend([lambda: pe_rows(g), lambda: park_rows(g)])
 
         def chore():
@@ -178,6 +190,7 @@ def tile_scaleddotproductattention_t_kernel(tc, x, out):
                 chores.remove(chores[0])
 
         def load_ri(b):
+            assert GROUP_OF[b][0] in parked
             ri = work4.tile([P, N], F32, name="RI")
             nc.sync.dma_start(out=ri[:], in_=park[b * N : (b + 1) * N].partition_broadcast(P))
             RI[b] = ri
@@ -195,6 +208,12 @@ def tile_scaleddotproductattention_t_kernel(tc, x, out):
             else:
                 nc.scalar.copy(out=xs[:], in_=xtp[:].rearrange("q t p -> q (t p)"))
             xT[b] = xs
+
+        def dummies(b):
+            dm = gps.tile([P, N], F32, name="dg")
+            xv = xT[b][:].bitcast(BF16)
+            for k in range(DUMMIES):
+                nc.tensor.matmul(dm[:], lhsT=xv[:, 0:P], rhs=xv[:, 0:N], start=True, stop=True)
 
         def pe_scores(b, rows):
             xv = xT[b][:].bitcast(BF16).rearrange("q (n e) -> q n e", e=2)
@@ -242,26 +261,32 @@ def tile_scaleddotproductattention_t_kernel(tc, x, out):
 
         def exp_direct(b):
             et = work3.tile([P, T, N], BF16, name="E")
-            r = small.tile([P, T], F32, name="rs")
+            k = b % 2 if b < PAIRS else 0
+            if k == 0:
+                rs[b] = small.tile([P, 2, T], F32, name="rs")
+                rm[b] = small.tile([P, 2, T], F32, name="rm")
+            r = rs[b - k][:, k, :]
             for t in range(T):
                 nc.scalar.activation(
                     out=et[:, t, t * P :], in_=S[b][t][:], func=ACTF.Exp, bias=-1.0, scale=1.0,
                     accum_out=r[:, t : t + 1],
                 )
             E[b] = et
-            rs[b] = r
 
         def exp_mirror(b):
-            r = small.tile([P, T - 1], F32, name="rm")
+            k = b % 2 if b < PAIRS else 0
+            r = rm[b - k][:, k, :]
             for t in (2, 1, 3):
                 nc.scalar.activation(
                     out=E[b][:, t, : t * P], in_=TB[b][t], func=ACTF.Exp, bias=-1.0, scale=1.0,
-                    accum_out=r[:, t - 1 : t],
+                    accum_out=r[:, t : t + 1],
                 )
-            rm[b] = r
 
         def add_sums(b):
-            nc.vector.tensor_tensor(out=rs[b][:, 1:], in0=rs[b][:, 1:], in1=rm[b][:], op=ALU.add)
+            n = 2 if b < PAIRS else 1
+            nc.vector.tensor_tensor(
+                out=rs[b][:, :n, 1:], in0=rs[b][:, :n, 1:], in1=rm[b][:, :n, 1:], op=ALU.add
+            )
 
         def x_regroup(b):
             xg = work2.tile([P, D, T], BF16, name="xg", align_bytes=64)
@@ -302,9 +327,11 @@ def tile_scaleddotproductattention_t_kernel(tc, x, out):
             eq[b] = (w, sc)
 
         def recip(b):
-            r = small.tile([P, T], F32, name="rinv")
-            nc.vector.reciprocal(out=r[:], in_=rs[b][:])
-            rinv[b] = r
+            n = 2 if b < PAIRS else 1
+            r = small.tile([P, 2, T], F32, name="rinv")
+            nc.vector.reciprocal(out=r[:, :n, :], in_=rs[b][:, :n, :])
+            for k in range(n):
+                rinv[b + k] = r[:, k, :]
 
         def pe_mx(b):
             w, sc = eq[b]
@@ -350,38 +377,42 @@ def tile_scaleddotproductattention_t_kernel(tc, x, out):
                     )
             nc.sync.dma_start(out=out[b].rearrange("(r c) d -> r c d", c=T), in_=o[:])
 
-        for b in range(-LB, B + 2):
-            if live(b + LD - 2):
-                queue_norms(b + LD - 2)
-            if live(b - 2):
-                add_sums(b - 2)
+        for b in range(-LD0, B + 2):
+            for g in range(EARLY, len(LOAD_GROUPS)):
+                if b == LOAD_AT[g - EARLY]:
+                    load_x(g)
+            for n in squared(b - 2):
+                queue_norms(n)
             chore()
             if live(b + LX):
                 xgs[b + LX] = x_regroup(b + LX)
             chore()
+            if live(b - 2) and (b % 2 == 0 or b - 2 >= PAIRS):
+                add_sums(b - 2)
             if live(b + LX - 1):
                 x_quant(b + LX - 1, xgs[b + LX - 1])
             chore()
+            if live(b - 2) and (b % 2 == 0 or b - 2 >= PAIRS):
+                recip(b - 2)
             if live(b + LR):
                 load_ri(b + LR)
             if live(b - 2):
-                recip(b - 2)
                 e_quant(b - 2, egs[b - 2])
+            if 0 <= b < TAIL:
+                dummies(b)
             if live(b + LB):
                 xtp = pe_xt(b + LB)
-            if live(b + LD) and b + LD >= SQ_S:
-                dg = pe_diag(b + LD)
             if live(b - 2):
                 banks = pe_mx(b - 2)
             if live(b - 1):
-                egs[b - 1] = e_regroup(b - 1, b - 1 == B - 1)
+                egs[b - 1] = e_regroup(b - 1, regroup_on_vector(b - 1))
             if live(b):
                 vec_scale(b)
-            if live(b + 1):
-                pe_scores(b + 1, [0])
             if live(b):
                 pe_mirror(b)
                 exp_direct(b)
+            if live(b + 1):
+                pe_scores(b + 1, [0])
             if live(b + 1):
                 pe_scores(b + 1, [1, 3])
             if live(b):
@@ -390,10 +421,7 @@ def tile_scaleddotproductattention_t_kernel(tc, x, out):
                 pe_scores(b + 1, [2])
             if live(b + LB):
                 copy_xt(b + LB, xtp)
-            if live(b + LD):
-                if b + LD < SQ_S:
-                    sumsq(b + LD)
-                else:
-                    vec_diag(b + LD, dg)
+            for n in squared(b):
+                sumsq(n)
             if live(b - 2):
                 finish(b - 2, banks)

@@ -18,17 +18,18 @@ P = 128
 B, N, D = 32, 512, 256
 T = N // P
 FLOPS = 2 * (2 * B * N * N * D)
-LD0 = 10
-LB = 3
-LX = 10
-LR = 1
-XT_V = 0
-GROUPS = [2, 5, 5, 7, 9, 4]
+LB = 2
+LR = 2
+NDIRECT = 3
+NFIRST = 8
+SQ0 = 10
+GROUPS = [NFIRST, 4, 6, 8, 6]
 GROUP_OF = [(g, k) for g, nb in enumerate(GROUPS) for k in range(nb)]
 FIRST = [sum(GROUPS[:g]) for g in range(len(GROUPS))]
-TAIL = B - 12
-PAIRS = B - 12
-DUMMIES = 1
+PREP0 = 12
+TAIL = B - 4
+PAIRS = B - 10
+QL = 2
 SEED = 1597463007.0
 LOAD_GROUPS = [1, 1, 2, 4, 4, 4, 4, 4, 4, 4]
 EARLY = 5
@@ -39,16 +40,28 @@ def fin_on_scalar(b, h):
     return h == 0 and b >= TAIL
 
 
+def xt_on_vector(b):
+    return False
+
+
 def regroup_on_vector(b):
     return b == B - 1
 
 
 def squared_by(b):
-    return max(0, min(B, b + LD0 + 1 + max(0, (b + 1) // 3)))
+    return max(0, min(B, b + SQ0 + 1 + max(0, (b + 1) * 2 // 5)))
 
 
 def squared(b):
     return range(squared_by(b - 1), squared_by(b))
+
+
+def prepared_by(b):
+    return max(0, min(B, (b + SQ0 + 1) * PREP0 // SQ0 if b < 0 else PREP0 + b + 1))
+
+
+def prepared(b):
+    return range(prepared_by(b - 1), prepared_by(b))
 
 
 def tile_scaleddotproductattention_t_kernel(tc, x, out):
@@ -60,8 +73,10 @@ def tile_scaleddotproductattention_t_kernel(tc, x, out):
         norms = ctx.enter_context(tc.tile_pool(name="norms", bufs=1))
         small = ctx.enter_context(tc.tile_pool(name="small", bufs=8))
         one = ctx.enter_context(tc.tile_pool(name="one", bufs=1))
-        deep = ctx.enter_context(tc.tile_pool(name="deep", bufs=15))
+        deep = ctx.enter_context(tc.tile_pool(name="deep", bufs=25))
+        xts = ctx.enter_context(tc.tile_pool(name="xts", bufs=4))
         work2 = ctx.enter_context(tc.tile_pool(name="work2", bufs=2))
+        xgp = ctx.enter_context(tc.tile_pool(name="xgp", bufs=6))
         work3 = ctx.enter_context(tc.tile_pool(name="work3", bufs=3))
         work4 = ctx.enter_context(tc.tile_pool(name="work4", bufs=4))
         gps = ctx.enter_context(tc.psum_pool(name="gps", bufs=1))
@@ -88,10 +103,11 @@ def tile_scaleddotproductattention_t_kernel(tc, x, out):
 
         ident = const.tile([P, P], F32, name="ident")
         make_identity(nc, ident[:])
-        mhalf = const.tile([P, GROUPS[0] * T], F32, name="mhalf")
-        nc.vector.memset(mhalf[:], -0.5)
         rna = const.tile([P, B * T], F32, name="rna")
         nc.vector.memset(rna[:], 1.0)
+        warm = const.tile([P, 2], F32, name="warm")
+        nc.vector.memset(warm[:], 1.0)
+        nc.scalar.activation(out=warm[:, 1:2], in_=warm[:, 0:1], func=ACTF.Abs_reciprocal_sqrt)
         park = out[B - 1].rearrange("n d -> (n d)")
 
         nsq = {}
@@ -125,6 +141,11 @@ def tile_scaleddotproductattention_t_kernel(tc, x, out):
                     out=junk[:], in_=xb3[b][:, t, :], func=ACTF.Square, accum_out=q[:, t : t + 1]
                 )
 
+        def first_guess(g):
+            y0 = newt.tile([P, GROUPS[g] * T], F32, name="yf")
+            nc.scalar.activation(out=y0[:], in_=nsq[g][:], func=ACTF.Abs_reciprocal_sqrt)
+            guess[g] = y0[:]
+
         def newton(g, step):
             q = nsq[g]
             w = GROUPS[g] * T
@@ -154,6 +175,8 @@ def tile_scaleddotproductattention_t_kernel(tc, x, out):
                     out=y, in0=part[g], scalar=1.5, in1=guess[g], op0=ALU.add, op1=ALU.mult
                 )
                 guess[g] = y
+                if step == 9:
+                    pe_rows(g)
 
         def pe_rows(g):
             rows = gps.tile([P, P], F32, name="dg")
@@ -169,25 +192,29 @@ def tile_scaleddotproductattention_t_kernel(tc, x, out):
                 out=park[r0 * P : r1 * P].rearrange("(r p) -> r p", p=P), in_=rt[r0:r1, :]
             )
 
-        def power(g):
-            w = GROUPS[g] * T
-            nc.gpsimd.tensor_tensor(
-                out=rna[:, FIRST[g] * T : FIRST[g] * T + w], in0=nsq[g][:], in1=mhalf[:, :w], op=ALU.pow
-            )
-
         def queue_norms(b):
             g, k = GROUP_OF[b]
             if k == GROUPS[g] - 1:
                 if g == 0:
-                    power(g)
-                else:
-                    chores.extend([lambda step=step: newton(g, step) for step in range(10)])
-                chores.extend([lambda: pe_rows(g), lambda: park_rows(g)])
+                    first_guess(g)
+                chores.extend([lambda step=step: newton(g, step) for step in range(7 if g == 0 else 0, 10)])
+                chores.extend([lambda: None, lambda: park_rows(g)])
 
         def chore():
             if chores:
                 chores[0]()
                 chores.remove(chores[0])
+
+        def pe_ri(b):
+            rip = gps.tile([P, T, P], F32, name="dg")
+            for c in range(T):
+                nc.tensor.transpose(rip[:, c, :], rna[:, b * T + c : b * T + c + 1].to_broadcast([P, P]), ident[:])
+            return rip
+
+        def copy_ri(b, rip):
+            ri = work4.tile([P, N], F32, name="RI")
+            nc.vector.tensor_copy(out=ri[:], in_=rip[:].rearrange("q t p -> q (t p)"))
+            RI[b] = ri
 
         def load_ri(b):
             assert GROUP_OF[b][0] in parked
@@ -202,18 +229,12 @@ def tile_scaleddotproductattention_t_kernel(tc, x, out):
             return xtp
 
         def copy_xt(b, xtp):
-            xs = deep.tile([P, T * P], F32, name="xT")
-            if b < XT_V:
+            xs = xts.tile([P, T * P], F32, name="xT")
+            if xt_on_vector(b):
                 nc.vector.tensor_copy(out=xs[:], in_=xtp[:].rearrange("q t p -> q (t p)"))
             else:
                 nc.scalar.copy(out=xs[:], in_=xtp[:].rearrange("q t p -> q (t p)"))
             xT[b] = xs
-
-        def dummies(b):
-            dm = gps.tile([P, N], F32, name="dg")
-            xv = xT[b][:].bitcast(BF16)
-            for k in range(DUMMIES):
-                nc.tensor.matmul(dm[:], lhsT=xv[:, 0:P], rhs=xv[:, 0:N], start=True, stop=True)
 
         def pe_scores(b, rows):
             xv = xT[b][:].bitcast(BF16).rearrange("q (n e) -> q n e", e=2)
@@ -289,7 +310,7 @@ def tile_scaleddotproductattention_t_kernel(tc, x, out):
             )
 
         def x_regroup(b):
-            xg = work2.tile([P, D, T], BF16, name="xg", align_bytes=64)
+            xg = xgp.tile([P, D, T], BF16, name="xg", align_bytes=64)
             nc.vector.tensor_copy(
                 out=xg[:].rearrange("p (c i) t -> p c t i", i=4),
                 in_=xb3[b].rearrange("p t (c i) -> p c t i", i=4),
@@ -377,51 +398,52 @@ def tile_scaleddotproductattention_t_kernel(tc, x, out):
                     )
             nc.sync.dma_start(out=out[b].rearrange("(r c) d -> r c d", c=T), in_=o[:])
 
-        for b in range(-LD0, B + 2):
+        for b in range(-SQ0, B + QL):
             for g in range(EARLY, len(LOAD_GROUPS)):
                 if b == LOAD_AT[g - EARLY]:
                     load_x(g)
-            for n in squared(b - 2):
-                queue_norms(n)
+            for n in squared(b - (1 if b < 0 else 2)):
+                if n < NFIRST or b >= 0:
+                    queue_norms(n)
             chore()
-            if live(b + LX):
-                xgs[b + LX] = x_regroup(b + LX)
+            for n in prepared(b):
+                xgs[n] = x_regroup(n)
             chore()
-            if live(b - 2) and (b % 2 == 0 or b - 2 >= PAIRS):
-                add_sums(b - 2)
-            if live(b + LX - 1):
-                x_quant(b + LX - 1, xgs[b + LX - 1])
+            for n in prepared(b - 1):
+                x_quant(n, xgs[n])
             chore()
-            if live(b - 2) and (b % 2 == 0 or b - 2 >= PAIRS):
-                recip(b - 2)
-            if live(b + LR):
+            if live(b - QL) and ((b - QL) % 2 == 0 or b - QL >= PAIRS):
+                add_sums(b - QL)
+            if live(b + LR) and b + LR >= NDIRECT:
                 load_ri(b + LR)
-            if live(b - 2):
-                e_quant(b - 2, egs[b - 2])
-            if 0 <= b < TAIL:
-                dummies(b)
+            if live(b - QL):
+                e_quant(b - QL, egs[b - QL])
+            if live(b - QL) and ((b - QL) % 2 == 0 or b - QL >= PAIRS):
+                recip(b - QL)
             if live(b + LB):
                 xtp = pe_xt(b + LB)
-            if live(b - 2):
-                banks = pe_mx(b - 2)
-            if live(b - 1):
-                egs[b - 1] = e_regroup(b - 1, regroup_on_vector(b - 1))
+            if live(b + 1) and b + 1 < NDIRECT:
+                rip = pe_ri(b + 1)
+            if live(b - QL):
+                banks = pe_mx(b - QL)
+            if live(b - QL + 1):
+                egs[b - QL + 1] = e_regroup(b - QL + 1, regroup_on_vector(b - QL + 1))
             if live(b):
                 vec_scale(b)
-            if live(b):
                 pe_mirror(b)
                 exp_direct(b)
             if live(b + 1):
                 pe_scores(b + 1, [0])
-            if live(b + 1):
                 pe_scores(b + 1, [1, 3])
             if live(b):
                 exp_mirror(b)
             if live(b + 1):
                 pe_scores(b + 1, [2])
+            if live(b + 1) and b + 1 < NDIRECT:
+                copy_ri(b + 1, rip)
             if live(b + LB):
                 copy_xt(b + LB, xtp)
             for n in squared(b):
                 sumsq(n)
-            if live(b - 2):
-                finish(b - 2, banks)
+            if live(b - QL):
+                finish(b - QL, banks)

@@ -18,18 +18,20 @@ P = 128
 B, N, D = 32, 512, 256
 T = N // P
 FLOPS = 2 * (2 * B * N * N * D)
-LB = 2
+LB = 3
 LR = 2
-NDIRECT = 3
+NDIRECT = 4
 NFIRST = 8
-SQ0 = 10
-GROUPS = [NFIRST, 4, 6, 8, 6]
+NONES = 4
+SQ0 = 11
+CHUNK = 4
+GROUPS = [NFIRST, 4, 4, 8, 8]
 GROUP_OF = [(g, k) for g, nb in enumerate(GROUPS) for k in range(nb)]
 FIRST = [sum(GROUPS[:g]) for g in range(len(GROUPS))]
-PREP0 = 12
-TAIL = B - 4
-PAIRS = B - 10
-QL = 2
+PREP0 = 15
+TAIL = B - 2
+PAIRS = B - 2
+QL = 3
 SEED = 1597463007.0
 LOAD_GROUPS = [1, 1, 2, 4, 4, 4, 4, 4, 4, 4]
 EARLY = 5
@@ -41,7 +43,7 @@ def fin_on_scalar(b, h):
 
 
 def xt_on_vector(b):
-    return False
+    return b % 3 == 1 and b < 22
 
 
 def regroup_on_vector(b):
@@ -74,7 +76,7 @@ def tile_scaleddotproductattention_t_kernel(tc, x, out):
         small = ctx.enter_context(tc.tile_pool(name="small", bufs=8))
         one = ctx.enter_context(tc.tile_pool(name="one", bufs=1))
         deep = ctx.enter_context(tc.tile_pool(name="deep", bufs=25))
-        xts = ctx.enter_context(tc.tile_pool(name="xts", bufs=4))
+        xts = ctx.enter_context(tc.tile_pool(name="xts", bufs=6))
         work2 = ctx.enter_context(tc.tile_pool(name="work2", bufs=2))
         xgp = ctx.enter_context(tc.tile_pool(name="xgp", bufs=6))
         work3 = ctx.enter_context(tc.tile_pool(name="work3", bufs=3))
@@ -123,6 +125,7 @@ def tile_scaleddotproductattention_t_kernel(tc, x, out):
         eq = {}
         rinv = {}
         chores = []
+        half = {}
         parked = []
         guess = {}
         part = {}
@@ -198,7 +201,7 @@ def tile_scaleddotproductattention_t_kernel(tc, x, out):
                 if g == 0:
                     first_guess(g)
                 chores.extend([lambda step=step: newton(g, step) for step in range(7 if g == 0 else 0, 10)])
-                chores.extend([lambda: None, lambda: park_rows(g)])
+                chores.extend([lambda: None] * NONES + [lambda: park_rows(g)])
 
         def chore():
             if chores:
@@ -214,13 +217,14 @@ def tile_scaleddotproductattention_t_kernel(tc, x, out):
         def copy_ri(b, rip):
             ri = work4.tile([P, N], F32, name="RI")
             nc.vector.tensor_copy(out=ri[:], in_=rip[:].rearrange("q t p -> q (t p)"))
-            RI[b] = ri
+            RI[b] = ri[:]
 
         def load_ri(b):
             assert GROUP_OF[b][0] in parked
-            ri = work4.tile([P, N], F32, name="RI")
-            nc.sync.dma_start(out=ri[:], in_=park[b * N : (b + 1) * N].partition_broadcast(P))
-            RI[b] = ri
+            ri = work3.tile([P, CHUNK * N], F32, name="RI4")
+            nc.sync.dma_start(out=ri[:], in_=park[b * N : (b + CHUNK) * N].partition_broadcast(P))
+            for k in range(CHUNK):
+                RI[b + k] = ri[:, k * N : (k + 1) * N]
 
         def pe_xt(b):
             xtp = gps.tile([P, T, P], F32, name="xtp")
@@ -241,15 +245,14 @@ def tile_scaleddotproductattention_t_kernel(tc, x, out):
             if rows[0] == 0:
                 ga = gps.tile([P, N], F32, name="ga")
                 G[b] = {0: ga[:]}
-                TB[b] = {}
             elif rows[0] == 1:
                 gb = gps.tile([P, N], F32, name="gb")
                 G[b][1] = gb[:, 0 : 3 * P]
                 G[b][3] = gb[:, 3 * P : 4 * P]
             else:
                 gc = gps.tile([P, N], F32, name="gc")
-                G[b][2] = gc[:, 0 : 2 * P]
-                TB[b][2] = gc[:, 2 * P : 4 * P]
+                G[b][2] = gc[:, : 2 * P]
+                half[b] = gc[:, 2 * P :]
             for t in rows:
                 for e in range(2):
                     nc.tensor.matmul(
@@ -272,8 +275,7 @@ def tile_scaleddotproductattention_t_kernel(tc, x, out):
 
         def pe_mirror(b):
             td = gps.tile([P, N], F32, name="td")
-            TB[b][1] = td[:, 0:P]
-            TB[b][3] = td[:, P:]
+            TB[b] = {1: td[:, 0:P], 2: half[b], 3: td[:, P:]}
             for t in range(T - 1):
                 for u in range(t + 1, T):
                     nc.tensor.transpose(
@@ -281,7 +283,7 @@ def tile_scaleddotproductattention_t_kernel(tc, x, out):
                     )
 
         def exp_direct(b):
-            et = work3.tile([P, T, N], BF16, name="E")
+            et = work4.tile([P, T, N], BF16, name="E")
             k = b % 2 if b < PAIRS else 0
             if k == 0:
                 rs[b] = small.tile([P, 2, T], F32, name="rs")
@@ -398,6 +400,7 @@ def tile_scaleddotproductattention_t_kernel(tc, x, out):
                     )
             nc.sync.dma_start(out=out[b].rearrange("(r c) d -> r c d", c=T), in_=o[:])
 
+        left = []
         for b in range(-SQ0, B + QL):
             for g in range(EARLY, len(LOAD_GROUPS)):
                 if b == LOAD_AT[g - EARLY]:
@@ -414,14 +417,13 @@ def tile_scaleddotproductattention_t_kernel(tc, x, out):
             chore()
             if live(b - QL) and ((b - QL) % 2 == 0 or b - QL >= PAIRS):
                 add_sums(b - QL)
-            if live(b + LR) and b + LR >= NDIRECT:
+            chore()
+            if live(b + LR) and b + LR >= NDIRECT and (b + LR) % CHUNK == 0:
                 load_ri(b + LR)
             if live(b - QL):
                 e_quant(b - QL, egs[b - QL])
             if live(b - QL) and ((b - QL) % 2 == 0 or b - QL >= PAIRS):
                 recip(b - QL)
-            if live(b + LB):
-                xtp = pe_xt(b + LB)
             if live(b + 1) and b + 1 < NDIRECT:
                 rip = pe_ri(b + 1)
             if live(b - QL):
@@ -430,20 +432,28 @@ def tile_scaleddotproductattention_t_kernel(tc, x, out):
                 egs[b - QL + 1] = e_regroup(b - QL + 1, regroup_on_vector(b - QL + 1))
             if live(b):
                 vec_scale(b)
+            for n, xtp in left:
+                copy_xt(n, xtp)
+            left.clear()
+            if live(b):
                 pe_mirror(b)
                 exp_direct(b)
             if live(b + 1):
                 pe_scores(b + 1, [0])
                 pe_scores(b + 1, [1, 3])
+            if live(b + LB):
+                xtp = pe_xt(b + LB)
             if live(b):
                 exp_mirror(b)
             if live(b + 1):
                 pe_scores(b + 1, [2])
             if live(b + 1) and b + 1 < NDIRECT:
                 copy_ri(b + 1, rip)
-            if live(b + LB):
+            if live(b + LB) and not xt_on_vector(b + LB):
                 copy_xt(b + LB, xtp)
             for n in squared(b):
                 sumsq(n)
             if live(b - QL):
                 finish(b - QL, banks)
+            if live(b + LB) and xt_on_vector(b + LB):
+                left.append((b + LB, xtp))

@@ -18,17 +18,17 @@ P = 128
 B, N, D = 32, 512, 256
 T = N // P
 FLOPS = 2 * (2 * B * N * N * D)
-LB = 3
-LR = 2
+LB = 2
 NDIRECT = 4
 NFIRST = 8
-NONES = 4
+NONES = 3
 SQ0 = 11
 CHUNK = 4
-GROUPS = [NFIRST, 4, 4, 8, 8]
+GROUPS = [NFIRST, 4, 4, 4, 4, 8]
 GROUP_OF = [(g, k) for g, nb in enumerate(GROUPS) for k in range(nb)]
 FIRST = [sum(GROUPS[:g]) for g in range(len(GROUPS))]
 PREP0 = 15
+LR = 4
 TAIL = B - 2
 PAIRS = B - 2
 QL = 3
@@ -43,7 +43,7 @@ def fin_on_scalar(b, h):
 
 
 def xt_on_vector(b):
-    return b % 3 == 1 and b < 22
+    return b % 4 > 0 and b < 16
 
 
 def regroup_on_vector(b):
@@ -220,8 +220,7 @@ def tile_scaleddotproductattention_t_kernel(tc, x, out):
             RI[b] = ri[:]
 
         def load_ri(b):
-            assert GROUP_OF[b][0] in parked
-            ri = work3.tile([P, CHUNK * N], F32, name="RI4")
+            ri = work4.tile([P, CHUNK * N], F32, name="RI4")
             nc.sync.dma_start(out=ri[:], in_=park[b * N : (b + CHUNK) * N].partition_broadcast(P))
             for k in range(CHUNK):
                 RI[b + k] = ri[:, k * N : (k + 1) * N]
@@ -401,6 +400,7 @@ def tile_scaleddotproductattention_t_kernel(tc, x, out):
             nc.sync.dma_start(out=out[b].rearrange("(r c) d -> r c d", c=T), in_=o[:])
 
         left = []
+        loaded = []
         for b in range(-SQ0, B + QL):
             for g in range(EARLY, len(LOAD_GROUPS)):
                 if b == LOAD_AT[g - EARLY]:
@@ -418,8 +418,10 @@ def tile_scaleddotproductattention_t_kernel(tc, x, out):
             if live(b - QL) and ((b - QL) % 2 == 0 or b - QL >= PAIRS):
                 add_sums(b - QL)
             chore()
-            if live(b + LR) and b + LR >= NDIRECT and (b + LR) % CHUNK == 0:
-                load_ri(b + LR)
+            for n in range(NDIRECT, B, CHUNK):
+                if n not in loaded and b >= n - LR and GROUP_OF[n][0] in parked:
+                    loaded.append(n)
+                    load_ri(n)
             if live(b - QL):
                 e_quant(b - QL, egs[b - QL])
             if live(b - QL) and ((b - QL) % 2 == 0 or b - QL >= PAIRS):

@@ -24,6 +24,7 @@ NFIRST = 8
 NONES = 3
 SQ0 = 11
 CHUNK = 4
+COPIES = 16
 GROUPS = [NFIRST, 4, 4, 4, 4, 8]
 GROUP_OF = [(g, k) for g, nb in enumerate(GROUPS) for k in range(nb)]
 FIRST = [sum(GROUPS[:g]) for g in range(len(GROUPS))]
@@ -110,7 +111,9 @@ def tile_scaleddotproductattention_t_kernel(tc, x, out):
         warm = const.tile([P, 2], F32, name="warm")
         nc.vector.memset(warm[:], 1.0)
         nc.scalar.activation(out=warm[:, 1:2], in_=warm[:, 0:1], func=ACTF.Abs_reciprocal_sqrt)
-        park = out[B - 1].rearrange("n d -> (n d)")
+        copies = out[B - 3 : B].rearrange("b n d -> (b n d)")[: COPIES * (B + 1) * N].rearrange(
+            "(c k) -> c k", c=COPIES
+        )
 
         nsq = {}
         xT = {}
@@ -192,7 +195,8 @@ def tile_scaleddotproductattention_t_kernel(tc, x, out):
             nc.vector.tensor_copy(out=rt[:], in_=part[g][:])
             r0, r1 = FIRST[g] * T, (FIRST[g] + GROUPS[g]) * T
             nc.sync.dma_start(
-                out=park[r0 * P : r1 * P].rearrange("(r p) -> r p", p=P), in_=rt[r0:r1, :]
+                out=copies[:, r0 * P : r1 * P].rearrange("c (r p) -> r c p", p=P),
+                in_=rt[r0:r1, :].unsqueeze(1).to_broadcast([r1 - r0, COPIES, P]),
             )
 
         def queue_norms(b):
@@ -221,7 +225,8 @@ def tile_scaleddotproductattention_t_kernel(tc, x, out):
 
         def load_ri(b):
             ri = work4.tile([P, CHUNK * N], F32, name="RI4")
-            nc.sync.dma_start(out=ri[:], in_=park[b * N : (b + CHUNK) * N].partition_broadcast(P))
+            for c in range(P // COPIES):
+                nc.sync.dma_start(out=ri[c : P : P // COPIES, :], in_=copies[:, b * N : (b + CHUNK) * N])
             for k in range(CHUNK):
                 RI[b + k] = ri[:, k * N : (k + 1) * N]
 

@@ -1,6 +1,5 @@
 from contextlib import ExitStack
 
-import concourse.bass as bass
 import concourse.mybir as mybir
 import concourse.tile as tile
 from concourse.masks import make_identity
@@ -8,7 +7,6 @@ from concourse.masks import make_identity
 F32 = mybir.dt.float32
 BF16 = mybir.dt.bfloat16
 U32 = mybir.dt.uint32
-I32 = mybir.dt.int32
 U8 = mybir.dt.uint8
 FP8X4 = mybir.dt.float8_e4m3fn_x4
 ALU = mybir.AluOpType
@@ -18,360 +16,261 @@ P = 128
 B, N, D = 32, 512, 256
 T = N // P
 FLOPS = 2 * (2 * B * N * N * D)
-LB = 2
-NDIRECT = 4
-NFIRST = 8
-NONES = 3
-SQ0 = 11
-CHUNK = 4
-COPIES = 16
-GROUPS = [NFIRST, 4, 4, 4, 4, 8]
-GROUP_OF = [(g, k) for g, nb in enumerate(GROUPS) for k in range(nb)]
-FIRST = [sum(GROUPS[:g]) for g in range(len(GROUPS))]
-PREP0 = 15
-LR = 4
-TAIL = B - 2
-PAIRS = B - 2
-QL = 3
-SEED = 1597463007.0
-LOAD_GROUPS = [1, 1, 2, 4, 4, 4, 4, 4, 4, 4]
-EARLY = 5
-LOAD_AT = [-5, -2, 0, 2, 5]
 
-
-def fin_on_scalar(b, h):
-    return h == 0 and b >= TAIL
-
-
-def xt_on_vector(b):
-    return b % 4 > 0 and b < 16
-
-
-def regroup_on_vector(b):
-    return b == B - 1
-
-
-def squared_by(b):
-    return max(0, min(B, b + SQ0 + 1 + max(0, (b + 1) * 2 // 5)))
-
-
-def squared(b):
-    return range(squared_by(b - 1), squared_by(b))
-
-
-def prepared_by(b):
-    return max(0, min(B, (b + SQ0 + 1) * PREP0 // SQ0 if b < 0 else PREP0 + b + 1))
-
-
-def prepared(b):
-    return range(prepared_by(b - 1), prepared_by(b))
+PREP = 8
+XT_LEAD = 2
+LAG = 3
+GROUP = 4
+FIRST_LOADS = [1, 1, 2, 4, 4]
+LOAD_LEAD = 16
+GP_COLS = 400
+XT_ON_VECTOR = 16
+LAST = B - 2
 
 
 def tile_scaleddotproductattention_t_kernel(tc, x, out):
     nc = tc.nc
     with ExitStack() as ctx:
         const = ctx.enter_context(tc.tile_pool(name="const", bufs=1))
-        xres = ctx.enter_context(tc.tile_pool(name="xres", bufs=1))
-        newt = ctx.enter_context(tc.tile_pool(name="newt", bufs=2))
-        norms = ctx.enter_context(tc.tile_pool(name="norms", bufs=1))
-        small = ctx.enter_context(tc.tile_pool(name="small", bufs=8))
-        one = ctx.enter_context(tc.tile_pool(name="one", bufs=1))
-        deep = ctx.enter_context(tc.tile_pool(name="deep", bufs=25))
-        xts = ctx.enter_context(tc.tile_pool(name="xts", bufs=6))
+        small = ctx.enter_context(tc.tile_pool(name="small", bufs=10))
+        xq_pool = ctx.enter_context(tc.tile_pool(name="xq_pool", bufs=PREP + LAG + 3))
+        work1 = ctx.enter_context(tc.tile_pool(name="work1", bufs=1))
         work2 = ctx.enter_context(tc.tile_pool(name="work2", bufs=2))
-        xgp = ctx.enter_context(tc.tile_pool(name="xgp", bufs=6))
         work3 = ctx.enter_context(tc.tile_pool(name="work3", bufs=3))
         work4 = ctx.enter_context(tc.tile_pool(name="work4", bufs=4))
-        gps = ctx.enter_context(tc.psum_pool(name="gps", bufs=1))
+        psum = ctx.enter_context(tc.psum_pool(name="psum", bufs=1))
         ctx.enter_context(tc.manual_schedule())
 
-        xb3 = []
-        xbw = []
-        def load_x(g):
-            nb = LOAD_GROUPS[g]
-            b0 = sum(LOAD_GROUPS[:g])
-            xt = xres.tile([P, nb * T * D], BF16, name="x%d" % g)
+        x_bf = []
+        x_word = []
+
+        def load_x(nb):
+            b0 = len(x_bf)
+            xt = const.tile([P, nb * T * D], BF16, name="x%d" % b0)
             nc.sync.dma_start(
                 out=xt[:].rearrange("p (k n) -> p k n", n=T * D),
                 in_=x[b0 : b0 + nb].rearrange("b (p t) d -> p b (t d)", t=T),
             )
-            v3 = xt[:].rearrange("p (k t d) -> p k t d", t=T, d=D)
-            vw = xt[:].bitcast(F32)
+            rows = xt[:].rearrange("p (k t d) -> p k t d", t=T, d=D)
+            words = xt[:].bitcast(F32).rearrange("p (k n) -> p k n", k=nb)
             for k in range(nb):
-                xb3.append(v3[:, k])
-                xbw.append(vw[:, k * (T * D // 2) : (k + 1) * (T * D // 2)])
+                x_bf.append(rows[:, k])
+                x_word.append(words[:, k])
 
-        for g in range(EARLY):
-            load_x(g)
+        for nb in FIRST_LOADS:
+            load_x(nb)
 
         ident = const.tile([P, P], F32, name="ident")
         make_identity(nc, ident[:])
-        rna = const.tile([P, B * T], F32, name="rna")
-        nc.vector.memset(rna[:], 1.0)
-        warm = const.tile([P, 2], F32, name="warm")
-        nc.vector.memset(warm[:], 1.0)
-        nc.scalar.activation(out=warm[:, 1:2], in_=warm[:, 0:1], func=ACTF.Abs_reciprocal_sqrt)
-        copies = out[B - 3 : B].rearrange("b n d -> (b n d)")[: COPIES * (B + 1) * N].rearrange(
-            "(c k) -> c k", c=COPIES
-        )
+        minus_half = const.tile([P, T], F32, name="minus_half")
+        nc.vector.memset(minus_half[:], -0.5)
+        rnorm = const.tile([P, B * T], F32, name="rnorm")
+        nc.vector.memset(rnorm[:], 1.0)
+        park = out[B - 1].rearrange("n d -> (n d)")
 
-        nsq = {}
-        xT = {}
-        RI = {}
-        xq = {}
-        G = {}
-        S = {}
-        TB = {}
-        rm = {}
-        E = {}
-        rs = {}
-        eq = {}
-        rinv = {}
-        chores = []
-        half = {}
-        parked = []
-        guess = {}
-        part = {}
+        nsq, xt_copy, factors, xg, xq = {}, {}, {}, {}, {}
+        scores, scaled, mirror, e, sums, mirror_sums, rinv = {}, {}, {}, {}, {}, {}, {}
+        eg, eq = {}, {}
+        pending = []
 
-        def nsq_cols(b):
-            g, k = GROUP_OF[b]
-            if k == 0:
-                nsq[g] = norms.tile([P, GROUPS[g] * T], F32, name="nsq%d" % g)
-            return nsq[g][:, k * T : (k + 1) * T]
+        def live(b):
+            return 0 <= b < B
 
-        def sumsq(b):
-            q = nsq_cols(b)
+
+        def sum_squares(b):
+            nsq[b] = small.tile([P, T], F32, name="nsq")
             for t in range(T):
                 junk = work2.tile([P, D], BF16, name="junk")
                 nc.scalar.activation(
-                    out=junk[:], in_=xb3[b][:, t, :], func=ACTF.Square, accum_out=q[:, t : t + 1]
+                    out=junk[:], in_=x_bf[b][:, t, :], func=ACTF.Square, accum_out=nsq[b][:, t : t + 1]
                 )
 
-        def first_guess(g):
-            y0 = newt.tile([P, GROUPS[g] * T], F32, name="yf")
-            nc.scalar.activation(out=y0[:], in_=nsq[g][:], func=ACTF.Abs_reciprocal_sqrt)
-            guess[g] = y0[:]
-
-        def newton(g, step):
-            q = nsq[g]
-            w = GROUPS[g] * T
-            if step == 0:
-                y0 = newt.tile([P, w], I32, name="y0")
-                nc.vector.tensor_scalar(
-                    out=y0[:], in0=q[:].bitcast(I32), scalar1=-0.5, scalar2=SEED, op0=ALU.mult, op1=ALU.add
-                )
-                guess[g] = y0[:].bitcast(F32)
-            elif step % 3 == 1:
-                u = newt.tile([P, w], F32, name="u")
-                nc.vector.scalar_tensor_tensor(
-                    out=u[:], in0=guess[g], scalar=-0.5, in1=guess[g], op0=ALU.mult, op1=ALU.mult
-                )
-                part[g] = u[:]
-            elif step % 3 == 2:
-                v = newt.tile([P, w], F32, name="v")
-                nc.vector.tensor_tensor(out=v[:], in0=part[g], in1=q[:], op=ALU.mult)
-                part[g] = v[:]
-            else:
-                if step < 9:
-                    y = newt.tile([P, w], F32, name="y%d" % step)
-                    y = y[:]
-                else:
-                    y = rna[:, FIRST[g] * T : FIRST[g] * T + w]
-                nc.vector.scalar_tensor_tensor(
-                    out=y, in0=part[g], scalar=1.5, in1=guess[g], op0=ALU.add, op1=ALU.mult
-                )
-                guess[g] = y
-                if step == 9:
-                    pe_rows(g)
-
-        def pe_rows(g):
-            rows = gps.tile([P, P], F32, name="dg")
-            nc.tensor.transpose(rows[:], rna[:], ident[:])
-            part[g] = rows
-
-        def park_rows(g):
-            parked.append(g)
-            rt = work2.tile([P, P], F32, name="rt")
-            nc.vector.tensor_copy(out=rt[:], in_=part[g][:])
-            r0, r1 = FIRST[g] * T, (FIRST[g] + GROUPS[g]) * T
-            nc.sync.dma_start(
-                out=copies[:, r0 * P : r1 * P].rearrange("c (r p) -> r c p", p=P),
-                in_=rt[r0:r1, :].unsqueeze(1).to_broadcast([r1 - r0, COPIES, P]),
+        def invert_norms(b):
+            nc.gpsimd.tensor_tensor(
+                out=rnorm[:, b * T : (b + 1) * T], in0=nsq[b][:], in1=minus_half[:], op=ALU.pow
             )
 
-        def queue_norms(b):
-            g, k = GROUP_OF[b]
-            if k == GROUPS[g] - 1:
-                if g == 0:
-                    first_guess(g)
-                chores.extend([lambda step=step: newton(g, step) for step in range(7 if g == 0 else 0, 10)])
-                chores.extend([lambda: None] * NONES + [lambda: park_rows(g)])
+        def transpose_rnorm():
+            rows = psum.tile([P, P], F32, name="rows")
+            nc.tensor.transpose(rows[:], rnorm[:], ident[:])
+            return rows
 
-        def chore():
-            if chores:
-                chores[0]()
-                chores.remove(chores[0])
+        def spread_group(b, rows):
+            copy = work2.tile([P, P], F32, name="rows_copy")
+            nc.vector.tensor_copy(out=copy[:], in_=rows[:])
+            spot = park[b * N : (b + GROUP) * N]
+            nc.sync.dma_start(
+                out=spot.rearrange("(r p) -> r p", p=P), in_=copy[b * T : (b + GROUP) * T, :]
+            )
+            f = work4.tile([P, GROUP, N], F32, name="factors4")
+            nc.sync.dma_start(out=f[:].rearrange("p b n -> p (b n)"), in_=spot.partition_broadcast(P))
+            for k in range(GROUP):
+                factors[b + k] = f[:, k, :]
 
-        def pe_ri(b):
-            rip = gps.tile([P, T, P], F32, name="dg")
-            for c in range(T):
-                nc.tensor.transpose(rip[:, c, :], rna[:, b * T + c : b * T + c + 1].to_broadcast([P, P]), ident[:])
-            return rip
-
-        def copy_ri(b, rip):
-            ri = work4.tile([P, N], F32, name="RI")
-            nc.vector.tensor_copy(out=ri[:], in_=rip[:].rearrange("q t p -> q (t p)"))
-            RI[b] = ri[:]
-
-        def load_ri(b):
-            ri = work4.tile([P, CHUNK * N], F32, name="RI4")
-            for c in range(P // COPIES):
-                nc.sync.dma_start(out=ri[c : P : P // COPIES, :], in_=copies[:, b * N : (b + CHUNK) * N])
-            for k in range(CHUNK):
-                RI[b + k] = ri[:, k * N : (k + 1) * N]
-
-        def pe_xt(b):
-            xtp = gps.tile([P, T, P], F32, name="xtp")
+        def spread_directly(b):
+            sp = psum.tile([P, T, P], F32, name="o0")
             for t in range(T):
-                nc.tensor.transpose(xtp[:, t, :], xbw[b][:, t * P : (t + 1) * P], ident[:])
-            return xtp
+                c = b * T + t
+                nc.tensor.transpose(sp[:, t, :], rnorm[:, c : c + 1].to_broadcast([P, P]), ident[:])
+            return sp
 
-        def copy_xt(b, xtp):
-            xs = xts.tile([P, T * P], F32, name="xT")
-            if xt_on_vector(b):
-                nc.vector.tensor_copy(out=xs[:], in_=xtp[:].rearrange("q t p -> q (t p)"))
-            else:
-                nc.scalar.copy(out=xs[:], in_=xtp[:].rearrange("q t p -> q (t p)"))
-            xT[b] = xs
+        def copy_spread(b, sp):
+            f = work4.tile([P, N], F32, name="factors1")
+            nc.vector.tensor_copy(out=f[:], in_=sp[:].rearrange("p t n -> p (t n)"))
+            factors[b] = f[:]
 
-        def pe_scores(b, rows):
-            xv = xT[b][:].bitcast(BF16).rearrange("q (n e) -> q n e", e=2)
-            if rows[0] == 0:
-                ga = gps.tile([P, N], F32, name="ga")
-                G[b] = {0: ga[:]}
-            elif rows[0] == 1:
-                gb = gps.tile([P, N], F32, name="gb")
-                G[b][1] = gb[:, 0 : 3 * P]
-                G[b][3] = gb[:, 3 * P : 4 * P]
-            else:
-                gc = gps.tile([P, N], F32, name="gc")
-                G[b][2] = gc[:, : 2 * P]
-                half[b] = gc[:, 2 * P :]
-            for t in rows:
-                for e in range(2):
-                    nc.tensor.matmul(
-                        G[b][t],
-                        lhsT=xv[:, t * P : (t + 1) * P, e],
-                        rhs=xv[:, t * P :, e],
-                        start=(e == 0),
-                        stop=(e == 1),
-                    )
 
-        def vec_scale(b):
-            S[b] = []
+        def transpose_x(b):
+            xp = psum.tile([P, T, P], F32, name="xp")
             for t in range(T):
-                s = work2.tile([P, (T - t) * P], F32, name="s%d" % t)
+                nc.tensor.transpose(xp[:, t, :], x_word[b][:, t * P : (t + 1) * P], ident[:])
+            return xp
+
+        def on_vector(b):
+            return b % 3 == 0 and b < XT_ON_VECTOR
+
+        def copy_x(b, xp):
+            xc = work4.tile([P, T * P], F32, name="xc")
+            if on_vector(b):
+                nc.vector.tensor_copy(out=xc[:], in_=xp[:].rearrange("q t p -> q (t p)"))
+            else:
+                nc.scalar.copy(out=xc[:], in_=xp[:].rearrange("q t p -> q (t p)"))
+            xt_copy[b] = xc
+
+        def score(b, t):
+            xh = xt_copy[b][:].bitcast(BF16).rearrange("q (n h) -> q n h", h=2)
+            for h in range(2):
+                nc.tensor.matmul(
+                    scores[b][t],
+                    lhsT=xh[:, t * P : (t + 1) * P, h],
+                    rhs=xh[:, t * P :, h],
+                    start=(h == 0),
+                    stop=(h == 1),
+                )
+
+        def score_first(b):
+            g0 = psum.tile([P, N], F32, name="g0")
+            g1 = psum.tile([P, N], F32, name="g1")
+            scores[b] = {0: g0[:], 1: g1[:, : 3 * P], 3: g1[:, 3 * P :]}
+            for t in (0, 1, 3):
+                score(b, t)
+
+        def score_last(b):
+            g2 = psum.tile([P, N], F32, name="g2")
+            scores[b][2] = g2[:, : 2 * P]
+            mirror[b] = {2: g2[:, 2 * P :]}
+            score(b, 2)
+
+        def scale(b):
+            scaled[b] = []
+            for t in range(T):
+                s = work2.tile([P, N - t * P], F32, name="s%d" % t)
+                c = b * T + t
                 nc.vector.scalar_tensor_tensor(
-                    out=s[:], in0=G[b][t], scalar=rna[:, b * T + t : b * T + t + 1], in1=RI[b][:, t * P :],
+                    out=s[:], in0=scores[b][t], scalar=rnorm[:, c : c + 1], in1=factors[b][:, t * P :],
                     op0=ALU.mult, op1=ALU.mult,
                 )
-                S[b].append(s)
+                scaled[b].append(s)
 
-        def pe_mirror(b):
-            td = gps.tile([P, N], F32, name="td")
-            TB[b] = {1: td[:, 0:P], 2: half[b], 3: td[:, P:]}
+        def mirror_scaled(b):
+            m = psum.tile([P, N], F32, name="m")
+            mirror[b][1] = m[:, :P]
+            mirror[b][3] = m[:, P:]
             for t in range(T - 1):
                 for u in range(t + 1, T):
                     nc.tensor.transpose(
-                        TB[b][u][:, t * P : (t + 1) * P], S[b][t][:, (u - t) * P : (u - t + 1) * P], ident[:]
+                        mirror[b][u][:, t * P : (t + 1) * P],
+                        scaled[b][t][:, (u - t) * P : (u - t + 1) * P],
+                        ident[:],
                     )
 
-        def exp_direct(b):
-            et = work4.tile([P, T, N], BF16, name="E")
-            k = b % 2 if b < PAIRS else 0
-            if k == 0:
-                rs[b] = small.tile([P, 2, T], F32, name="rs")
-                rm[b] = small.tile([P, 2, T], F32, name="rm")
-            r = rs[b - k][:, k, :]
-            for t in range(T):
-                nc.scalar.activation(
-                    out=et[:, t, t * P :], in_=S[b][t][:], func=ACTF.Exp, bias=-1.0, scale=1.0,
-                    accum_out=r[:, t : t + 1],
-                )
-            E[b] = et
 
-        def exp_mirror(b):
-            k = b % 2 if b < PAIRS else 0
-            r = rm[b - k][:, k, :]
+        def pair(b):
+            return b % 2 if b < LAST else 0
+
+        def exp_part(b, t, cols, s, row_sum):
+            nc.scalar.activation(
+                out=e[b][:, t, cols], in_=s, func=ACTF.Exp, bias=-1.0, scale=1.0, accum_out=row_sum[:, t : t + 1]
+            )
+
+        def exp_direct(b):
+            e[b] = work4.tile([P, T, N], BF16, name="e")
+            k = pair(b)
+            if k == 0:
+                sums[b] = small.tile([P, 2, T], F32, name="sums")
+                mirror_sums[b] = small.tile([P, 2, T], F32, name="mirror_sums")
+            for t in range(T):
+                exp_part(b, t, slice(t * P, N), scaled[b][t][:], sums[b - k][:, k, :])
+
+        def exp_mirrored(b):
+            k = pair(b)
             for t in (2, 1, 3):
-                nc.scalar.activation(
-                    out=E[b][:, t, : t * P], in_=TB[b][t], func=ACTF.Exp, bias=-1.0, scale=1.0,
-                    accum_out=r[:, t : t + 1],
-                )
+                exp_part(b, t, slice(0, t * P), mirror[b][t], mirror_sums[b - k][:, k, :])
+
+        def opens_pair(b):
+            return live(b) and pair(b) == 0
 
         def add_sums(b):
-            n = 2 if b < PAIRS else 1
+            n = 2 if b < LAST else 1
             nc.vector.tensor_tensor(
-                out=rs[b][:, :n, 1:], in0=rs[b][:, :n, 1:], in1=rm[b][:, :n, 1:], op=ALU.add
+                out=sums[b][:, :n, 1:], in0=sums[b][:, :n, 1:], in1=mirror_sums[b][:, :n, 1:], op=ALU.add
             )
 
-        def x_regroup(b):
-            xg = xgp.tile([P, D, T], BF16, name="xg", align_bytes=64)
-            nc.vector.tensor_copy(
-                out=xg[:].rearrange("p (c i) t -> p c t i", i=4),
-                in_=xb3[b].rearrange("p t (c i) -> p c t i", i=4),
-            )
-            return xg
-
-        def x_quant(b, xg):
-            w = deep.tile([P, D], U32, name="xq", align_bytes=64)
-            sc = deep.tile([P, D], U8, name="xsc", align_bytes=64)
-            nc.vector.quantize_mx(
-                out=w[:].bitcast(FP8X4), scales=sc[:], in_=xg[:].rearrange("p d t -> p (d t)")
-            )
-            xq[b] = (w, sc)
-
-        def e_regroup(b, on_vector):
-            eg = one.tile([P, N, T], BF16, name="eg", align_bytes=64)
-            if on_vector:
-                nc.vector.tensor_copy(
-                    out=eg[:].rearrange("p (c i) t -> p c t i", i=4),
-                    in_=E[b][:].rearrange("p t (c i) -> p c t i", i=4),
-                )
-            else:
-                nc.gpsimd.tensor_scalar(
-                    out=eg[:], in0=E[b][:].rearrange("p t i -> p i t"),
-                    scalar1=1.0, scalar2=0.0, op0=ALU.mult, op1=ALU.add,
-                )
-            return eg
-
-        def e_quant(b, eg):
-            w = work2.tile([P, N], U32, name="eq", align_bytes=64)
-            sc = work2.tile([P, N], U8, name="esc", align_bytes=64)
-            nc.vector.quantize_mx(
-                out=w[:].bitcast(FP8X4), scales=sc[:], in_=eg[:].rearrange("p i t -> p (i t)")
-            )
-            eq[b] = (w, sc)
-
-        def recip(b):
-            n = 2 if b < PAIRS else 1
+        def invert_sums(b):
+            n = 2 if b < LAST else 1
             r = small.tile([P, 2, T], F32, name="rinv")
-            nc.vector.reciprocal(out=r[:, :n, :], in_=rs[b][:, :n, :])
+            nc.vector.reciprocal(out=r[:, :n, :], in_=sums[b][:, :n, :])
             for k in range(n):
                 rinv[b + k] = r[:, k, :]
 
-        def pe_mx(b):
-            w, sc = eq[b]
+
+        def regroup_on_vector(dst, src):
+            nc.vector.tensor_copy(
+                out=dst.rearrange("p (c i) t -> p c t i", i=4), in_=src.rearrange("p t (c i) -> p c t i", i=4)
+            )
+
+        def regroup_x(b):
+            xg[b] = work2.tile([P, D, T], BF16, name="xg", align_bytes=64)
+            regroup_on_vector(xg[b][:], x_bf[b])
+
+        def quantise_x(b):
+            w = xq_pool.tile([P, D], U32, name="xw", align_bytes=64)
+            sc = xq_pool.tile([P, D], U8, name="xsc", align_bytes=64)
+            nc.vector.quantize_mx(
+                out=w[:].bitcast(FP8X4), scales=sc[:], in_=xg[b][:].rearrange("p d t -> p (d t)")
+            )
+            xq[b] = (w, sc)
+
+        def regroup_e(b):
+            eg[b] = work1.tile([P, N, T], BF16, name="eg", align_bytes=64)
+            m = GP_COLS if b < LAST else 0
+            regroup_on_vector(eg[b][:, m:, :], e[b][:, :, m:])
+            if m:
+                nc.gpsimd.tensor_scalar(
+                    out=eg[b][:, :m, :], in0=e[b][:, :, :m].rearrange("p t i -> p i t"),
+                    scalar1=1.0, scalar2=0.0, op0=ALU.mult, op1=ALU.add,
+                )
+
+        def quantise_e(b):
+            w = work2.tile([P, N], U32, name="ew", align_bytes=64)
+            sc = work2.tile([P, N], U8, name="esc", align_bytes=64)
+            nc.vector.quantize_mx(
+                out=w[:].bitcast(FP8X4), scales=sc[:], in_=eg[b][:].rearrange("p i t -> p (i t)")
+            )
+            eq[b] = (w, sc)
+
+        def multiply(b):
+            ew, esc = eq[b]
             xw, xsc = xq[b]
             banks = []
             for h in range(2):
-                o = gps.tile([P, 2, D], F32, name="op%d" % h)
+                o = psum.tile([P, 2, D], F32, name="o%d" % h)
                 for k in range(2):
-                    c = 2 * h + k
+                    q = slice((2 * h + k) * P, (2 * h + k + 1) * P)
                     nc.tensor.matmul_mx(
                         out=o[:, k, :],
-                        lhsT=w[:, c * P : (c + 1) * P].bitcast(FP8X4),
-                        lhsT_scale=sc[:, c * P : (c + 1) * P],
+                        lhsT=ew[:, q].bitcast(FP8X4),
+                        lhsT_scale=esc[:, q],
                         rhs=xw[:].bitcast(FP8X4),
                         rhs_scale=xsc[:],
                         start=True,
@@ -380,87 +279,78 @@ def tile_scaleddotproductattention_t_kernel(tc, x, out):
                 banks.append(o)
             return banks
 
-        xgs = {}
-        egs = {}
-
-        def live(b):
-            return 0 <= b < B
-
         def finish(b, banks):
             o = work3.tile([P, T, D], F32, name="o")
             for h in range(2):
-                if fin_on_scalar(b, h):
+                c = 2 * h
+                if h == 0 and b >= LAST:
                     for k in range(2):
-                        c = 2 * h + k
                         nc.scalar.activation(
-                            out=o[:, c, :], in_=banks[h][:, k, :], func=ACTF.Copy,
-                            scale=rinv[b][:, c : c + 1],
+                            out=o[:, c + k, :], in_=banks[h][:, k, :], func=ACTF.Copy,
+                            scale=rinv[b][:, c + k : c + k + 1],
                         )
                 else:
                     nc.vector.tensor_tensor(
-                        out=o[:, 2 * h : 2 * h + 2, :], in0=banks[h][:],
-                        in1=rinv[b][:, 2 * h : 2 * h + 2].unsqueeze(2).to_broadcast([P, 2, D]),
-                        op=ALU.mult,
+                        out=o[:, c : c + 2, :], in0=banks[h][:],
+                        in1=rinv[b][:, c : c + 2].unsqueeze(2).to_broadcast([P, 2, D]), op=ALU.mult,
                     )
-            nc.sync.dma_start(out=out[b].rearrange("(r c) d -> r c d", c=T), in_=o[:])
+            nc.sync.dma_start(out=out[b].rearrange("(p t) d -> p t d", t=T), in_=o[:])
 
-        left = []
-        loaded = []
-        for b in range(-SQ0, B + QL):
-            for g in range(EARLY, len(LOAD_GROUPS)):
-                if b == LOAD_AT[g - EARLY]:
-                    load_x(g)
-            for n in squared(b - (1 if b < 0 else 2)):
-                if n < NFIRST or b >= 0:
-                    queue_norms(n)
-            chore()
-            for n in prepared(b):
-                xgs[n] = x_regroup(n)
-            chore()
-            for n in prepared(b - 1):
-                x_quant(n, xgs[n])
-            chore()
-            if live(b - QL) and ((b - QL) % 2 == 0 or b - QL >= PAIRS):
-                add_sums(b - QL)
-            chore()
-            for n in range(NDIRECT, B, CHUNK):
-                if n not in loaded and b >= n - LR and GROUP_OF[n][0] in parked:
-                    loaded.append(n)
-                    load_ri(n)
-            if live(b - QL):
-                e_quant(b - QL, egs[b - QL])
-            if live(b - QL) and ((b - QL) % 2 == 0 or b - QL >= PAIRS):
-                recip(b - QL)
-            if live(b + 1) and b + 1 < NDIRECT:
-                rip = pe_ri(b + 1)
-            if live(b - QL):
-                banks = pe_mx(b - QL)
-            if live(b - QL + 1):
-                egs[b - QL + 1] = e_regroup(b - QL + 1, regroup_on_vector(b - QL + 1))
+        for b in range(-PREP, B + LAG):
+            behind = b - LAG
+            ahead = b + PREP
+            if live(b + LOAD_LEAD) and b + LOAD_LEAD >= sum(FIRST_LOADS) and b % GROUP == 0:
+                load_x(GROUP)
+
+            if live(ahead):
+                regroup_x(ahead)
+            last = ahead - 2
+            spread = live(last) and last >= GROUP and last % GROUP == GROUP - 1
+            if spread:
+                rows = transpose_rnorm()
+            if live(ahead - 1):
+                quantise_x(ahead - 1)
+            if opens_pair(behind):
+                add_sums(behind)
+            if live(behind):
+                quantise_e(behind)
+            if opens_pair(behind):
+                invert_sums(behind)
+            if live(b + 1) and b + 1 < GROUP:
+                sp = spread_directly(b + 1)
+            if live(behind):
+                banks = multiply(behind)
+
+            if live(behind + 1):
+                regroup_e(behind + 1)
+            if live(ahead - 1):
+                invert_norms(ahead - 1)
+
             if live(b):
-                vec_scale(b)
-            for n, xtp in left:
-                copy_xt(n, xtp)
-            left.clear()
+                scale(b)
+            if spread:
+                spread_group(last - GROUP + 1, rows)
+            while pending:
+                copy_x(*pending.pop())
             if live(b):
-                pe_mirror(b)
+                mirror_scaled(b)
                 exp_direct(b)
             if live(b + 1):
-                pe_scores(b + 1, [0])
-                pe_scores(b + 1, [1, 3])
-            if live(b + LB):
-                xtp = pe_xt(b + LB)
+                score_first(b + 1)
+            if live(b + XT_LEAD):
+                xp = transpose_x(b + XT_LEAD)
             if live(b):
-                exp_mirror(b)
+                exp_mirrored(b)
             if live(b + 1):
-                pe_scores(b + 1, [2])
-            if live(b + 1) and b + 1 < NDIRECT:
-                copy_ri(b + 1, rip)
-            if live(b + LB) and not xt_on_vector(b + LB):
-                copy_xt(b + LB, xtp)
-            for n in squared(b):
-                sumsq(n)
-            if live(b - QL):
-                finish(b - QL, banks)
-            if live(b + LB) and xt_on_vector(b + LB):
-                left.append((b + LB, xtp))
+                score_last(b + 1)
+            if live(b + 1) and b + 1 < GROUP:
+                copy_spread(b + 1, sp)
+            if live(b + XT_LEAD):
+                if on_vector(b + XT_LEAD):
+                    pending.append((b + XT_LEAD, xp))
+                else:
+                    copy_x(b + XT_LEAD, xp)
+            if live(ahead):
+                sum_squares(ahead)
+            if live(behind):
+                finish(behind, banks)

from contextlib import ExitStack

import concourse.mybir as mybir
import concourse.tile as tile
from concourse.masks import make_identity

F32 = mybir.dt.float32
BF16 = mybir.dt.bfloat16
U32 = mybir.dt.uint32
U8 = mybir.dt.uint8
FP8X4 = mybir.dt.float8_e4m3fn_x4
ALU = mybir.AluOpType
ACTF = mybir.ActivationFunctionType

P = 128
B, N, D = 32, 512, 256
T = N // P
FLOPS = 2 * (2 * B * N * N * D)

PREP = 8
XT_LEAD = 2
LAG = 3
GROUP = 4
FIRST_LOADS = [1, 1, 2, 4, 4]
LOAD_LEAD = 16
GP_COLS = 400
XT_ON_VECTOR = 16
LAST = B - 2


def tile_scaleddotproductattention_t_kernel(tc, x, out):
    nc = tc.nc
    with ExitStack() as ctx:
        const = ctx.enter_context(tc.tile_pool(name="const", bufs=1))
        small = ctx.enter_context(tc.tile_pool(name="small", bufs=10))
        xq_pool = ctx.enter_context(tc.tile_pool(name="xq_pool", bufs=PREP + LAG + 3))
        work1 = ctx.enter_context(tc.tile_pool(name="work1", bufs=1))
        work2 = ctx.enter_context(tc.tile_pool(name="work2", bufs=2))
        work3 = ctx.enter_context(tc.tile_pool(name="work3", bufs=3))
        work4 = ctx.enter_context(tc.tile_pool(name="work4", bufs=4))
        psum = ctx.enter_context(tc.psum_pool(name="psum", bufs=1))
        ctx.enter_context(tc.manual_schedule())

        x_bf = []
        x_word = []

        def load_x(nb):
            b0 = len(x_bf)
            xt = const.tile([P, nb * T * D], BF16, name="x%d" % b0)
            nc.sync.dma_start(
                out=xt[:].rearrange("p (k n) -> p k n", n=T * D),
                in_=x[b0 : b0 + nb].rearrange("b (p t) d -> p b (t d)", t=T),
            )
            rows = xt[:].rearrange("p (k t d) -> p k t d", t=T, d=D)
            words = xt[:].bitcast(F32).rearrange("p (k n) -> p k n", k=nb)
            for k in range(nb):
                x_bf.append(rows[:, k])
                x_word.append(words[:, k])

        for nb in FIRST_LOADS:
            load_x(nb)

        ident = const.tile([P, P], F32, name="ident")
        make_identity(nc, ident[:])
        minus_half = const.tile([P, T], F32, name="minus_half")
        nc.vector.memset(minus_half[:], -0.5)
        rnorm = const.tile([P, B * T], F32, name="rnorm")
        nc.vector.memset(rnorm[:], 1.0)
        park = out[B - 1].rearrange("n d -> (n d)")

        nsq, xt_copy, factors, xg, xq = {}, {}, {}, {}, {}
        scores, scaled, mirror, e, sums, mirror_sums, rinv = {}, {}, {}, {}, {}, {}, {}
        eg, eq = {}, {}
        pending = []

        def live(b):
            return 0 <= b < B


        def sum_squares(b):
            nsq[b] = small.tile([P, T], F32, name="nsq")
            for t in range(T):
                junk = work2.tile([P, D], BF16, name="junk")
                nc.scalar.activation(
                    out=junk[:], in_=x_bf[b][:, t, :], func=ACTF.Square, accum_out=nsq[b][:, t : t + 1]
                )

        def invert_norms(b):
            nc.gpsimd.tensor_tensor(
                out=rnorm[:, b * T : (b + 1) * T], in0=nsq[b][:], in1=minus_half[:], op=ALU.pow
            )

        def transpose_rnorm():
            rows = psum.tile([P, P], F32, name="rows")
            nc.tensor.transpose(rows[:], rnorm[:], ident[:])
            return rows

        def spread_group(b, rows):
            copy = work2.tile([P, P], F32, name="rows_copy")
            nc.vector.tensor_copy(out=copy[:], in_=rows[:])
            spot = park[b * N : (b + GROUP) * N]
            nc.sync.dma_start(
                out=spot.rearrange("(r p) -> r p", p=P), in_=copy[b * T : (b + GROUP) * T, :]
            )
            f = work4.tile([P, GROUP, N], F32, name="factors4")
            nc.sync.dma_start(out=f[:].rearrange("p b n -> p (b n)"), in_=spot.partition_broadcast(P))
            for k in range(GROUP):
                factors[b + k] = f[:, k, :]

        def spread_directly(b):
            sp = psum.tile([P, T, P], F32, name="o0")
            for t in range(T):
                c = b * T + t
                nc.tensor.transpose(sp[:, t, :], rnorm[:, c : c + 1].to_broadcast([P, P]), ident[:])
            return sp

        def copy_spread(b, sp):
            f = work4.tile([P, N], F32, name="factors1")
            nc.vector.tensor_copy(out=f[:], in_=sp[:].rearrange("p t n -> p (t n)"))
            factors[b] = f[:]


        def transpose_x(b):
            xp = psum.tile([P, T, P], F32, name="xp")
            for t in range(T):
                nc.tensor.transpose(xp[:, t, :], x_word[b][:, t * P : (t + 1) * P], ident[:])
            return xp

        def on_vector(b):
            return b % 3 == 0 and b < XT_ON_VECTOR

        def copy_x(b, xp):
            xc = work4.tile([P, T * P], F32, name="xc")
            if on_vector(b):
                nc.vector.tensor_copy(out=xc[:], in_=xp[:].rearrange("q t p -> q (t p)"))
            else:
                nc.scalar.copy(out=xc[:], in_=xp[:].rearrange("q t p -> q (t p)"))
            xt_copy[b] = xc

        def score(b, t):
            xh = xt_copy[b][:].bitcast(BF16).rearrange("q (n h) -> q n h", h=2)
            for h in range(2):
                nc.tensor.matmul(
                    scores[b][t],
                    lhsT=xh[:, t * P : (t + 1) * P, h],
                    rhs=xh[:, t * P :, h],
                    start=(h == 0),
                    stop=(h == 1),
                )

        def score_first(b):
            g0 = psum.tile([P, N], F32, name="g0")
            g1 = psum.tile([P, N], F32, name="g1")
            scores[b] = {0: g0[:], 1: g1[:, : 3 * P], 3: g1[:, 3 * P :]}
            for t in (0, 1, 3):
                score(b, t)

        def score_last(b):
            g2 = psum.tile([P, N], F32, name="g2")
            scores[b][2] = g2[:, : 2 * P]
            mirror[b] = {2: g2[:, 2 * P :]}
            score(b, 2)

        def scale(b):
            scaled[b] = []
            for t in range(T):
                s = work2.tile([P, N - t * P], F32, name="s%d" % t)
                c = b * T + t
                nc.vector.scalar_tensor_tensor(
                    out=s[:], in0=scores[b][t], scalar=rnorm[:, c : c + 1], in1=factors[b][:, t * P :],
                    op0=ALU.mult, op1=ALU.mult,
                )
                scaled[b].append(s)

        def mirror_scaled(b):
            m = psum.tile([P, N], F32, name="m")
            mirror[b][1] = m[:, :P]
            mirror[b][3] = m[:, P:]
            for t in range(T - 1):
                for u in range(t + 1, T):
                    nc.tensor.transpose(
                        mirror[b][u][:, t * P : (t + 1) * P],
                        scaled[b][t][:, (u - t) * P : (u - t + 1) * P],
                        ident[:],
                    )


        def pair(b):
            return b % 2 if b < LAST else 0

        def exp_part(b, t, cols, s, row_sum):
            nc.scalar.activation(
                out=e[b][:, t, cols], in_=s, func=ACTF.Exp, bias=-1.0, scale=1.0, accum_out=row_sum[:, t : t + 1]
            )

        def exp_direct(b):
            e[b] = work4.tile([P, T, N], BF16, name="e")
            k = pair(b)
            if k == 0:
                sums[b] = small.tile([P, 2, T], F32, name="sums")
                mirror_sums[b] = small.tile([P, 2, T], F32, name="mirror_sums")
            for t in range(T):
                exp_part(b, t, slice(t * P, N), scaled[b][t][:], sums[b - k][:, k, :])

        def exp_mirrored(b):
            k = pair(b)
            for t in (2, 1, 3):
                exp_part(b, t, slice(0, t * P), mirror[b][t], mirror_sums[b - k][:, k, :])

        def opens_pair(b):
            return live(b) and pair(b) == 0

        def add_sums(b):
            n = 2 if b < LAST else 1
            nc.vector.tensor_tensor(
                out=sums[b][:, :n, 1:], in0=sums[b][:, :n, 1:], in1=mirror_sums[b][:, :n, 1:], op=ALU.add
            )

        def invert_sums(b):
            n = 2 if b < LAST else 1
            r = small.tile([P, 2, T], F32, name="rinv")
            nc.vector.reciprocal(out=r[:, :n, :], in_=sums[b][:, :n, :])
            for k in range(n):
                rinv[b + k] = r[:, k, :]


        def regroup_on_vector(dst, src):
            nc.vector.tensor_copy(
                out=dst.rearrange("p (c i) t -> p c t i", i=4), in_=src.rearrange("p t (c i) -> p c t i", i=4)
            )

        def regroup_x(b):
            xg[b] = work2.tile([P, D, T], BF16, name="xg", align_bytes=64)
            regroup_on_vector(xg[b][:], x_bf[b])

        def quantise_x(b):
            w = xq_pool.tile([P, D], U32, name="xw", align_bytes=64)
            sc = xq_pool.tile([P, D], U8, name="xsc", align_bytes=64)
            nc.vector.quantize_mx(
                out=w[:].bitcast(FP8X4), scales=sc[:], in_=xg[b][:].rearrange("p d t -> p (d t)")
            )
            xq[b] = (w, sc)

        def regroup_e(b):
            eg[b] = work1.tile([P, N, T], BF16, name="eg", align_bytes=64)
            m = GP_COLS if b < LAST else 0
            regroup_on_vector(eg[b][:, m:, :], e[b][:, :, m:])
            if m:
                nc.gpsimd.tensor_scalar(
                    out=eg[b][:, :m, :], in0=e[b][:, :, :m].rearrange("p t i -> p i t"),
                    scalar1=1.0, scalar2=0.0, op0=ALU.mult, op1=ALU.add,
                )

        def quantise_e(b):
            w = work2.tile([P, N], U32, name="ew", align_bytes=64)
            sc = work2.tile([P, N], U8, name="esc", align_bytes=64)
            nc.vector.quantize_mx(
                out=w[:].bitcast(FP8X4), scales=sc[:], in_=eg[b][:].rearrange("p i t -> p (i t)")
            )
            eq[b] = (w, sc)

        def multiply(b):
            ew, esc = eq[b]
            xw, xsc = xq[b]
            banks = []
            for h in range(2):
                o = psum.tile([P, 2, D], F32, name="o%d" % h)
                for k in range(2):
                    q = slice((2 * h + k) * P, (2 * h + k + 1) * P)
                    nc.tensor.matmul_mx(
                        out=o[:, k, :],
                        lhsT=ew[:, q].bitcast(FP8X4),
                        lhsT_scale=esc[:, q],
                        rhs=xw[:].bitcast(FP8X4),
                        rhs_scale=xsc[:],
                        start=True,
                        stop=True,
                    )
                banks.append(o)
            return banks

        def finish(b, banks):
            o = work3.tile([P, T, D], F32, name="o")
            for h in range(2):
                c = 2 * h
                if h == 0 and b >= LAST:
                    for k in range(2):
                        nc.scalar.activation(
                            out=o[:, c + k, :], in_=banks[h][:, k, :], func=ACTF.Copy,
                            scale=rinv[b][:, c + k : c + k + 1],
                        )
                else:
                    nc.vector.tensor_tensor(
                        out=o[:, c : c + 2, :], in0=banks[h][:],
                        in1=rinv[b][:, c : c + 2].unsqueeze(2).to_broadcast([P, 2, D]), op=ALU.mult,
                    )
            nc.sync.dma_start(out=out[b].rearrange("(p t) d -> p t d", t=T), in_=o[:])

        for b in range(-PREP, B + LAG):
            behind = b - LAG
            ahead = b + PREP
            if live(b + LOAD_LEAD) and b + LOAD_LEAD >= sum(FIRST_LOADS) and b % GROUP == 0:
                load_x(GROUP)

            if live(ahead):
                regroup_x(ahead)
            last = ahead - 2
            spread = live(last) and last >= GROUP and last % GROUP == GROUP - 1
            if spread:
                rows = transpose_rnorm()
            if live(ahead - 1):
                quantise_x(ahead - 1)
            if opens_pair(behind):
                add_sums(behind)
            if live(behind):
                quantise_e(behind)
            if opens_pair(behind):
                invert_sums(behind)
            if live(b + 1) and b + 1 < GROUP:
                sp = spread_directly(b + 1)
            if live(behind):
                banks = multiply(behind)

            if live(behind + 1):
                regroup_e(behind + 1)
            if live(ahead - 1):
                invert_norms(ahead - 1)

            if live(b):
                scale(b)
            if spread:
                spread_group(last - GROUP + 1, rows)
            while pending:
                copy_x(*pending.pop())
            if live(b):
                mirror_scaled(b)
                exp_direct(b)
            if live(b + 1):
                score_first(b + 1)
            if live(b + XT_LEAD):
                xp = transpose_x(b + XT_LEAD)
            if live(b):
                exp_mirrored(b)
            if live(b + 1):
                score_last(b + 1)
            if live(b + 1) and b + 1 < GROUP:
                copy_spread(b + 1, sp)
            if live(b + XT_LEAD):
                if on_vector(b + XT_LEAD):
                    pending.append((b + XT_LEAD, xp))
                else:
                    copy_x(b + XT_LEAD, xp)
            if live(ahead):
                sum_squares(ahead)
            if live(behind):
                finish(behind, banks)
